import numpy as np
import ml_dtypes


def mxq(x, axis, fmt="e4m3"):
    dtype, down = {"e4m3": (ml_dtypes.float8_e4m3fn, 7), "e5m2": (ml_dtypes.float8_e5m2, 14)}[fmt]
    v = np.moveaxis(np.asarray(x, np.float32).astype(ml_dtypes.bfloat16).astype(np.float64), axis, -1)
    blocks = v.reshape(v.shape[:-1] + (-1, 32))
    amax = np.abs(blocks).max(-1, keepdims=True)
    byte = np.maximum(np.where(amax > 0, np.frexp(amax)[1] - 1 + 127, 0) - down, 1)
    scale = np.exp2(byte - 127.0)
    codes = (blocks / scale).astype(np.float32).astype(dtype).astype(np.float64)
    return np.moveaxis((codes * scale).reshape(v.shape), -1, axis)


WIDE = False


def mx_kscale(k):
    if not WIDE:
        return np.ones(k)
    levels = np.array([10, -10, 5, -5, 0])
    if k % 512:
        return np.exp2(np.random.permutation(np.resize(levels, k // 32))).repeat(32)
    a = np.empty((k // 512, 16))
    for p in range(k // 512):
        a[p, :8] = np.random.permutation(np.resize(levels, 8))
        for g in range(8):
            far = levels[np.abs(levels - a[p, g]) >= 10]
            a[p, g + 8] = far[np.random.randint(len(far))]
    return np.exp2(a.ravel()).repeat(32)


BF16 = ml_dtypes.bfloat16


def bf(x):
    return np.asarray(x, np.float32).astype(BF16)


def f64(x):
    return np.asarray(x).astype(np.float64)


B, T, H, DK, DH, E, V = 128, 1, 24, 64, 64, 1536, 1536
HK = H * DK


def rotate_every_two(u):
    u1 = u[..., ::2]
    u2 = u[..., 1::2]
    return np.stack((-u2, u1), axis=-1).reshape(u.shape)


def theta_shift(u, sin, cos):
    return u * cos + rotate_every_two(u) * sin


def draw0():
    s = mx_kscale(E)
    return {"x": bf(np.random.standard_normal((B, T, E)) * s),
            "sin": bf(np.random.standard_normal((T, DK)) * 0.7),
            "cos": bf(np.random.standard_normal((T, DK)) * 0.7),
            "Wq": bf(np.random.standard_normal((E, HK)) / np.sqrt(E) / s[:, None]),
            "Wk": bf(np.random.standard_normal((E, HK)) / np.sqrt(E) / s[:, None])}


def core(x, sin, cos, Wq, Wk):
    xq = mxq(f64(x), 2, "e4m3")
    q = (xq @ mxq(f64(Wq), 0, "e4m3")).reshape(B, T, H, DK).transpose(0, 2, 1, 3)
    k = (xq @ mxq(f64(Wk), 0, "e4m3")).reshape(B, T, H, DK).transpose(0, 2, 1, 3)
    qr = theta_shift(q, f64(sin), f64(cos))
    kr = theta_shift(k, f64(sin), f64(cos))
    return qr, kr


def e4m3fn_bytes(y):
    return np.clip(np.asarray(y, np.float64), -448.0, 448.0).astype(np.float32).astype(ml_dtypes.float8_e4m3fn).view(np.uint8)


def e4m3fn_values(b):
    return np.asarray(b, np.uint8).view(ml_dtypes.float8_e4m3fn).astype(np.float64)


def setup_inputs():
    d = draw0()
    x0 = np.asarray(d['Wq']).astype(np.float64)
    s = (np.max(np.abs(x0), axis=(1,), keepdims=True) / 448.0).astype(np.float32)
    out = {}
    for k, v in d.items():
        if k == 'Wq':
            out['Wq_bytes'] = e4m3fn_bytes(x0 / s.astype(np.float64))
            out['Wq_scale'] = s
        else:
            out[k] = v
    return out


def reference(x, sin, cos, Wq_bytes, Wq_scale, Wk):
    return core(x, sin, cos, e4m3fn_values(Wq_bytes) * Wq_scale.astype(np.float64), Wk)

@@ -1,0 +1,273 @@
+from contextlib import ExitStack
+
+import concourse.mybir as mybir
+from concourse.masks import make_identity
+
+F32 = mybir.dt.float32
+BF16 = mybir.dt.bfloat16
+U32 = mybir.dt.uint32
+U8 = mybir.dt.uint8
+FP8 = mybir.dt.float8_e4m3fn
+FP8X4 = mybir.dt.float8_e4m3fn_x4
+ACT = mybir.ActivationFunctionType
+ALU = mybir.AluOpType
+
+B = 128
+E = 1536
+HK = 1536
+DK = 64
+P = 128
+PACK = 4
+K_PASS = P * PACK
+PASSES = E // K_PASS
+CHUNK = 512
+CHUNKS = HK // CHUNK
+TILES = CHUNK // P
+
+FLOPS = 2 * 2 * B * E * HK
+
+ORDER = (
+    "Wq00 Wq01.0 Wq01.1 Iq00 Wq01.2 Wq01.3 Wq02.0 Iq01 xT Wq02.1 Wq02.2 Qq00 Wq02.3 Ik00 xE0 xE1 xE2 Qq01 "
+    "Wq10.0 Iq02 Wq10.1 Wq10.2 Qk00 Wq10.3 Iq10.0 Ik01 Iq10.1 xQ R Wq11.0 Qq02 Wq11.1 Qk01 M1q0 Wq11.2 "
+    "Ik02 Wq11.3 E1q0 Qq10 Wq12.0 M2q0 Wq12.1 Iq11 Wq12.2 E2q0 Qk02 Wq12.3 Ik10 M1k0 Wq20.0 Wq20.1 Qq11 "
+    "E1k0 Iq12 Wq20.2 M2k0 Wq20.3 Qk10 Wq21.0 Ik11 E2k0 Wq21.1 Qq12 Wq21.2 Wq21.3 Iq20 M1q1 Wq22.0 Qk11 "
+    "Wq22.1 E1q1 Ik12 Wq22.2 M2q1 Wq22.3 Qq20 Iq22.0 Iq21 E2q1 Qk12 Iq22.1 Qq21 M1k1 Ik20.0 Qq22 Ik21 "
+    "M1q2 E1k1 Ik20.1 M2k1 E1q2 Qk20 M2q2 I0 E2k1 I1 Q0 Qk21 E2q2 I2 M1pre Q1 I3 P0 Q2 P1 E1_0 Q3 P2 E1_1 "
+    "M2_0 E1_2 M2_1 E2_0 M2_2 E2_1 P3 E2_2 E1_3 M2_3 E2_3"
+)
+SEQ = "q00 q01 k00 q02 k01 q10 k02 q11 k10 q12 k11 q20 k12 q21 q22 k20 k21 k22"
+LOADS = "s q00 q01 k00 q02 x k01 q10 k02 c q11 k10 q12 k11 q20 k12 q21 q22 k20 k21 k22"
+
+
+def tile_multiscaleretention_pa_kernel(tc, x, sin, cos, Wq_bytes, Wq_scale, Wk, out_0, out_1):
+    nc = tc.nc
+    x2d = x.rearrange("b t e -> b (t e)")
+    outs = {
+        "q": out_0.rearrange("b h t d -> b (h t d)"),
+        "k": out_1.rearrange("b h t d -> b (h t d)"),
+    }
+    wk_view = Wk.rearrange("(g p t) n -> g p t n", p=P, t=PACK)
+    wq_view = Wq_bytes.rearrange("(g p t) n -> g p t n", p=P, t=PACK)
+
+    chunks = [(m, c) for c in range(CHUNKS) for m in ("q", "k")]
+    units = [(s[0], int(s[1]), int(s[2])) for s in SEQ.split()]
+
+    with ExitStack() as ctx:
+        keep = ctx.enter_context(tc.tile_pool(name="keep", bufs=1))
+        wide_pool = ctx.enter_context(tc.tile_pool(name="wide", bufs=5))
+        grp_pool = ctx.enter_context(tc.tile_pool(name="grp", bufs=4))
+        qt_pool = ctx.enter_context(tc.tile_pool(name="qt", bufs=3))
+        res_pool = ctx.enter_context(tc.tile_pool(name="res", bufs=9))
+        pst = ctx.enter_context(tc.psum_pool(name="pst", bufs=4))
+        ps1 = ctx.enter_context(tc.psum_pool(name="ps1", bufs=2))
+        ps2 = ctx.enter_context(tc.psum_pool(name="ps2", bufs=2))
+
+        raw = {}
+
+        def load(u):
+            m, c, g = u
+            cols = slice(c * CHUNK, (c + 1) * CHUNK)
+            if m == "k":
+                t = keep.tile([P, PACK, CHUNK], BF16, name="kraw%d%d" % (c, g))
+                nc.sync.dma_start(out=t[:], in_=wk_view[g][:, :, cols])
+            else:
+                t = keep.tile([P, PACK, CHUNK], U8, name="qbytes%d%d" % (c, g))
+                nc.sync.dma_start(out=t[:], in_=wq_view[g][:, :, cols])
+            raw[u] = t
+
+        scl = keep.tile([P, PASSES, PACK], F32, name="scl")
+        x_sb = keep.tile([P, E], BF16, name="x_sb")
+        cs = keep.tile([P, 2, DK], BF16, name="cs")
+
+        for s in LOADS.split():
+            if s == "s":
+                nc.sync.dma_start(out=scl[:], in_=Wq_scale.rearrange("(g p t) o -> p g (t o)", p=P, t=PACK))
+            elif s == "x":
+                nc.sync.dma_start(out=x_sb[:], in_=x2d)
+            elif s == "c":
+                nc.sync.dma_start(out=cs[:, 0, :], in_=cos.rearrange("o d -> (o d)").partition_broadcast(P))
+                nc.sync.dma_start(out=cs[:, 1, :], in_=sin.rearrange("o d -> (o d)").partition_broadcast(P))
+            else:
+                load((s[0], int(s[1]), int(s[2])))
+
+        idsw = keep.tile([P, 2, P], F32, name="idsw")
+        make_identity(nc, idsw[:, 0, :])
+        ident = idsw[:, 0, :]
+        id_pairs = idsw[:, 0, :].rearrange("p (i two) -> p i two", two=2)
+        sw_pairs = idsw[:, 1, :].rearrange("p (i two) -> p i two", two=2)
+        nc.gpsimd.tensor_scalar(out=sw_pairs[:, :, 0], in0=id_pairs[:, :, 1], scalar1=-1.0, scalar2=None, op0=ALU.mult)
+        nc.gpsimd.tensor_copy(out=sw_pairs[:, :, 1], in_=id_pairs[:, :, 0])
+
+        warm = keep.tile([P, 2], F32, name="warm")
+        nc.vector.memset(warm[:, 0:1], 0.0)
+        nc.scalar.activation(out=warm[:, 1:2], in_=warm[:, 0:1], func=ACT.Copy)
+
+        rot = keep.tile([P, P], F32, name="rot")
+        x_grp = keep.tile([P, PASSES, B * PACK], BF16, name="x_grp", align_bytes=64)
+        x_codes = keep.tile([P, PASSES, B], U32, name="x_codes", align_bytes=64)
+        x_scales = keep.tile([P, PASSES, B], U8, name="x_scales", align_bytes=64)
+
+        def build_rot():
+            prod = keep.tile([P, 2, P], F32, name="prod")
+            nc.vector.tensor_tensor(
+                out=prod[:].rearrange("p s (h d) -> p s h d", h=2),
+                in0=idsw[:].rearrange("p s (h d) -> p s h d", h=2),
+                in1=cs[:].unsqueeze(2).to_broadcast([P, 2, 2, DK]),
+                op=ALU.mult,
+            )
+            nc.vector.tensor_tensor(out=rot[:], in0=prod[:, 0, :], in1=prod[:, 1, :], op=ALU.add)
+
+        codes = {}
+        scales = {}
+        for ch in chunks:
+            codes[ch] = keep.tile([P, PASSES, CHUNK], U32, name="codes_%s%d" % ch, align_bytes=64)
+            scales[ch] = keep.tile([P, PASSES, CHUNK], U8, name="scales_%s%d" % ch, align_bytes=64)
+
+        wide = {}
+        grp = {}
+        acc = {}
+        qts = {}
+        turned = {}
+
+        def unit(s):
+            return (s[0], int(s[1]), int(s[2]))
+
+        def widen(u, t, on_vector):
+            if u not in wide:
+                w = wide_pool.tile([P, PACK, CHUNK], BF16, name="wide")
+                wide[u] = w
+            g = u[2]
+            if on_vector:
+                nc.vector.tensor_scalar(
+                    out=wide[u][:, t, :], in0=raw[u][:, t, :].bitcast(FP8), scalar1=scl[:, g, t : t + 1], scalar2=None, op0=ALU.mult
+                )
+            else:
+                nc.scalar.activation(
+                    out=wide[u][:, t, :], in_=raw[u][:, t, :].bitcast(FP8), func=ACT.Copy, scale=scl[:, g, t : t + 1]
+                )
+
+        def interleave(u, lo, hi, on_vector):
+            src = raw[u] if u[0] == "k" else wide[u]
+            if u not in grp:
+                gt = grp_pool.tile([P, CHUNK, PACK], BF16, name="grp", align_bytes=64)
+                grp[u] = gt
+            if on_vector:
+                nc.vector.tensor_copy(out=grp[u][:, lo:hi, :], in_=src[:, :, lo:hi].rearrange("p t n -> p n t"))
+            else:
+                nc.scalar.copy(out=grp[u][:, lo:hi, :], in_=src[:, :, lo:hi].rearrange("p t n -> p n t"))
+
+        def quantize(u, lo, hi):
+            m, c, g = u
+            nc.vector.quantize_mx(
+                out=codes[(m, c)][:, g, lo:hi].bitcast(FP8X4),
+                scales=scales[(m, c)][:, g, lo:hi],
+                in_=grp[u][:, lo:hi, :].rearrange("p n t -> p (n t)"),
+            )
+
+        def passes(ch, acc_cols, j, gs):
+            cols = slice(j * P, (j + 1) * P)
+            for g in gs:
+                nc.tensor.matmul_mx(
+                    out=acc_cols,
+                    lhsT=codes[ch][:, g, cols].bitcast(FP8X4),
+                    lhsT_scale=scales[ch][:, g, cols],
+                    rhs=x_codes[:, g, :].bitcast(FP8X4),
+                    rhs_scale=x_scales[:, g, :],
+                    start=(g == 0),
+                    stop=(g == PASSES - 1),
+                )
+
+        def copy_out(key, width):
+            qt = qt_pool.tile([P, CHUNK], F32, name="qt")
+            nc.scalar.copy(out=qt[:, :width], in_=acc[key][:, :width])
+            qts[key] = qt
+
+        def rotate(key, n_tiles):
+            tu = ps2.tile([P, CHUNK], F32, name="turned")
+            for j in range(n_tiles):
+                cols = slice(j * P, (j + 1) * P)
+                nc.tensor.matmul(out=tu[:, cols], lhsT=qts[key][:, cols], rhs=rot[:], start=True, stop=True)
+            turned[key] = tu
+
+        def store(key, ch, first_tile, n_tiles, on_vector):
+            m, c = ch
+            width = n_tiles * P
+            res = res_pool.tile([P, CHUNK], F32, name="res")
+            if on_vector:
+                nc.vector.tensor_copy(out=res[:, :width], in_=turned[key][:, :width])
+            else:
+                nc.scalar.copy(out=res[:, :width], in_=turned[key][:, :width])
+            lo = c * CHUNK + first_tile * P
+            nc.sync.dma_start(out=outs[m][:, lo : lo + width], in_=res[:, :width])
+
+        last = units[len(units) - 1]
+        last_ch = (last[0], last[1])
+        xts = {}
+        words = x_sb[:].bitcast(F32)
+
+        def run(tok):
+            if tok == "xT":
+                for g in range(PASSES):
+                    xt = pst.tile([P, 2, B], F32, name="xt", tag="bank")
+                    xts[g] = xt
+                    for u in range(2):
+                        nc.tensor.transpose(xt[:, u, :], words[:, 256 * g + u : 256 * (g + 1) : 2], ident)
+            elif tok.startswith("xE"):
+                g = int(tok[2])
+                nc.scalar.copy(
+                    out=x_grp[:, g, :].bitcast(F32).rearrange("p (b u) -> p b u", u=2),
+                    in_=xts[g][:].rearrange("p u b -> p b u"),
+                )
+            elif tok == "xQ":
+                for g in range(PASSES):
+                    nc.vector.quantize_mx(out=x_codes[:, g, :].bitcast(FP8X4), scales=x_scales[:, g, :], in_=x_grp[:, g, :])
+            elif tok == "R":
+                build_rot()
+            elif tok == "M1pre":
+                for j in range(TILES):
+                    acc_t = pst.tile([P, P], F32, name="acc_t", tag="bank")
+                    acc[j] = acc_t
+                    passes(last_ch, acc_t[:], j, range(PASSES - 1))
+            elif tok.startswith("M1"):
+                ch = (tok[2], int(tok[3]))
+                a = ps1.tile([P, CHUNK], F32, name="acc")
+                acc[ch] = a
+                for j in range(TILES):
+                    passes(ch, a[:, j * P : (j + 1) * P], j, range(PASSES))
+            elif tok.startswith("E1_"):
+                copy_out(int(tok[3]), P)
+            elif tok.startswith("M2_"):
+                rotate(int(tok[3]), 1)
+            elif tok.startswith("E2_"):
+                store(int(tok[3]), last_ch, int(tok[3]), 1, True)
+            elif tok.startswith("E1"):
+                copy_out((tok[2], int(tok[3])), CHUNK)
+            elif tok.startswith("M2"):
+                rotate((tok[2], int(tok[3])), TILES)
+            elif tok.startswith("E2"):
+                store((tok[2], int(tok[3])), (tok[2], int(tok[3])), 0, TILES, False)
+            elif tok.startswith("W"):
+                if len(tok) == 4:
+                    for t in range(PACK):
+                        widen(unit(tok[1:4]), t, True)
+                else:
+                    widen(unit(tok[1:4]), int(tok[5]), False)
+            elif tok.startswith("P"):
+                passes(last_ch, acc[int(tok[1])][:], int(tok[1]), [PASSES - 1])
+            elif tok.startswith("I") and len(tok) == 2:
+                interleave(last, int(tok[1]) * P, (int(tok[1]) + 1) * P, True)
+            elif tok.startswith("Q") and len(tok) == 2:
+                quantize(last, int(tok[1]) * P, (int(tok[1]) + 1) * P)
+            elif tok.startswith("I") and len(tok) == 4:
+                interleave(unit(tok[1:4]), 0, CHUNK, True)
+            elif tok.startswith("I"):
+                h = int(tok[5])
+                interleave(unit(tok[1:4]), h * CHUNK // 2, (h + 1) * CHUNK // 2, False)
+            elif tok.startswith("Q"):
+                quantize(unit(tok[1:4]), 0, CHUNK)
+            else:
+                raise ValueError(tok)
+
+        with tc.manual_schedule():
+            for tok in ORDER.split():
+                run(tok)

@@ -151,10 +151,12 @@ def tile_multiscaleretention_pa_kernel(tc, x, sin, cos, Wq_bytes, Wq_scale, Wk, 
             if u not in grp:
                 gt = grp_pool.tile([P, CHUNK, PACK], BF16, name="grp", align_bytes=64)
                 grp[u] = gt
+            dst_v = grp[u][:, lo:hi, :].rearrange("p (c i) t -> p c t i", i=4)
+            src_v = src[:, :, lo:hi].rearrange("p t (c i) -> p c t i", i=4)
             if on_vector:
-                nc.vector.tensor_copy(out=grp[u][:, lo:hi, :], in_=src[:, :, lo:hi].rearrange("p t n -> p n t"))
+                nc.vector.tensor_copy(out=dst_v, in_=src_v)
             else:
-                nc.scalar.copy(out=grp[u][:, lo:hi, :], in_=src[:, :, lo:hi].rearrange("p t n -> p n t"))
+                nc.scalar.copy(out=dst_v, in_=src_v)
 
         def quantize(u, lo, hi):
             m, c, g = u

@@ -27,16 +27,16 @@ TILES = CHUNK // P
 FLOPS = 2 * 2 * B * E * HK
 
 ORDER = (
-    "Wq00 Wq01.0 Wq01.1 Iq00 Wq01.2 Wq01.3 Wq02.0 Iq01 xT Wq02.1 Wq02.2 Qq00 Wq02.3 Ik00 xE0 xE1 xE2 Qq01 "
-    "Wq10.0 Iq02 Wq10.1 Wq10.2 Qk00 Wq10.3 Iq10.0 Ik01 Iq10.1 xQ R Wq11.0 Qq02 Wq11.1 Qk01 M1q0 Wq11.2 "
-    "Ik02 Wq11.3 E1q0 Qq10 Wq12.0 M2q0 Wq12.1 Iq11 Wq12.2 E2q0 Qk02 Wq12.3 Ik10 M1k0 Wq20.0 Wq20.1 Qq11 "
-    "E1k0 Iq12 Wq20.2 M2k0 Wq20.3 Qk10 Wq21.0 Ik11 E2k0 Wq21.1 Qq12 Wq21.2 Wq21.3 Iq20 M1q1 Wq22.0 Qk11 "
-    "Wq22.1 E1q1 Ik12 Wq22.2 M2q1 Wq22.3 Qq20 Iq22.0 Iq21 E2q1 Qk12 Iq22.1 Qq21 M1k1 Ik20.0 Qq22 Ik21 "
-    "M1q2 E1k1 Ik20.1 M2k1 E1q2 Qk20 M2q2 I0 E2k1 I1 Q0 Qk21 E2q2 I2 M1pre Q1 I3 P0 Q2 P1 E1_0 Q3 P2 E1_1 "
-    "M2_0 E1_2 M2_1 E2_0 M2_2 E2_1 P3 E2_2 E1_3 M2_3 E2_3"
+    "Wq00 Wq01.0 Wq01.1 Iq00 Wq01.2 Wq01.3 Wq02.0 Iq01 Wq02.1 xT Wq02.2 Qq00 Wq02.3 Ik00 Ik01.0 Qq01 xE0 "
+    "xE1 Iq02 xE2 Wq10.0 Ik01.1 Qk00 xQ Wq10.1 R Wq10.2 Qq02 Wq10.3 M1q0 Wq11.0 Iq10 Wq11.1 Wq11.2 Qk01 "
+    "Wq11.3 Ik02 E1q0 Wq12.0 M2q0 Qq10 Wq12.1 Iq11 Wq12.2 E2q0 Qk02 Wq12.3 Wq20.0 Ik10 M1k0 Wq20.1 Wq20.2 "
+    "Qq11 Wq20.3 Iq12 E1k0 Wq21.0 M2k0 Qk10 Wq21.1 Ik11 Wq21.2 Wq21.3 Qq12 Wq22.0 Iq20 E2k0 M1q1 Wq22.1 "
+    "Wq22.2 Qk11 E1q1 Ik12 Wq22.3 M2q1 Iq22.0 Qq20 Iq21 E2q1 Iq22.1 Qk12 Qq21 M1k1 Ik20.0 Qq22 Ik21 "
+    "Ik20.1 M1q2 E1k1 Qk20 E1q2 M2k1 I0 Qk21 I1 M2q2 E2k1 Q0 I2 Q1 Mpre0 I3 E2q2 Mpre1 Q2 P0 Q3 P1 P2 "
+    "E1_0 P3 E1_1 M2_0 E1_2 E1_3 M2_1 E2_0 M2_2 E2_1 M2_3 E2_2 E2_3"
 )
 SEQ = "q00 q01 k00 q02 k01 q10 k02 q11 k10 q12 k11 q20 k12 q21 q22 k20 k21 k22"
-LOADS = "s q00 q01 k00 q02 x k01 q10 k02 c q11 k10 q12 k11 q20 k12 q21 q22 k20 k21 k22"
+LOADS = "s q00 q01 k00 q02 x k01 q10 k02 q11 k10 c q12 k11 q20 k12 q21 q22 k20 k21 k22"
 
 
 def tile_multiscaleretention_pa_kernel(tc, x, sin, cos, Wq_bytes, Wq_scale, Wk, out_0, out_1):
@@ -54,8 +54,8 @@ def tile_multiscaleretention_pa_kernel(tc, x, sin, cos, Wq_bytes, Wq_scale, Wk, 
 
     with ExitStack() as ctx:
         keep = ctx.enter_context(tc.tile_pool(name="keep", bufs=1))
-        wide_pool = ctx.enter_context(tc.tile_pool(name="wide", bufs=5))
-        grp_pool = ctx.enter_context(tc.tile_pool(name="grp", bufs=4))
+        wide_pool = ctx.enter_context(tc.tile_pool(name="wide", bufs=9))
+        grp_pool = ctx.enter_context(tc.tile_pool(name="grp", bufs=6))
         qt_pool = ctx.enter_context(tc.tile_pool(name="qt", bufs=3))
         res_pool = ctx.enter_context(tc.tile_pool(name="res", bufs=9))
         pst = ctx.enter_context(tc.psum_pool(name="pst", bufs=4))
@@ -81,7 +81,7 @@ def tile_multiscaleretention_pa_kernel(tc, x, sin, cos, Wq_bytes, Wq_scale, Wk, 
 
         for s in LOADS.split():
             if s == "s":
-                nc.sync.dma_start(out=scl[:], in_=Wq_scale.rearrange("(g p t) o -> p g (t o)", p=P, t=PACK))
+                nc.scalar.dma_start(out=scl[:], in_=Wq_scale.rearrange("(g p t) o -> p g (t o)", p=P, t=PACK))
             elif s == "x":
                 nc.sync.dma_start(out=x_sb[:], in_=x2d)
             elif s == "c":
@@ -225,11 +225,13 @@ def tile_multiscaleretention_pa_kernel(tc, x, sin, cos, Wq_bytes, Wq_scale, Wk, 
                     nc.vector.quantize_mx(out=x_codes[:, g, :].bitcast(FP8X4), scales=x_scales[:, g, :], in_=x_grp[:, g, :])
             elif tok == "R":
                 build_rot()
-            elif tok == "M1pre":
+            elif tok.startswith("Mpre"):
+                g = int(tok[4])
                 for j in range(TILES):
-                    acc_t = pst.tile([P, P], F32, name="acc_t", tag="bank")
-                    acc[j] = acc_t
-                    passes(last_ch, acc_t[:], j, range(PASSES - 1))
+                    if g == 0:
+                        acc_t = pst.tile([P, P], F32, name="acc_t", tag="bank")
+                        acc[j] = acc_t
+                    passes(last_ch, acc[j][:], j, [g])
             elif tok.startswith("M1"):
                 ch = (tok[2], int(tok[3]))
                 a = ps1.tile([P, CHUNK], F32, name="acc")

@@ -151,8 +151,8 @@ def tile_multiscaleretention_pa_kernel(tc, x, sin, cos, Wq_bytes, Wq_scale, Wk, 
             if u not in grp:
                 gt = grp_pool.tile([P, CHUNK, PACK], BF16, name="grp", align_bytes=64)
                 grp[u] = gt
-            dst_v = grp[u][:, lo:hi, :].rearrange("p (c i) t -> p c t i", i=4)
-            src_v = src[:, :, lo:hi].rearrange("p t (c i) -> p c t i", i=4)
+            dst_v = grp[u][:, lo:hi, :].rearrange("p (c i) t -> p c t i", i=8)
+            src_v = src[:, :, lo:hi].rearrange("p t (c i) -> p c t i", i=8)
             if on_vector:
                 nc.vector.tensor_copy(out=dst_v, in_=src_v)
             else:

@@ -27,7 +27,7 @@ TILES = CHUNK // P
 FLOPS = 2 * 2 * B * E * HK
 
 ORDER = (
-    "Wq00 Wq01.0 Wq01.1 Iq00 Wq01.2 Wq01.3 Wq02.0 Iq01 Wq02.1 xT Wq02.2 Qq00 Wq02.3 Ik00 Ik01.0 Qq01 xE0 "
+    "Wq00 Wq01.0 Wq01.1 Iq00 Wq01.2 Wq01.3 Wq02.0 Iq01 Wq02.1 xT B Wq02.2 Qq00 Wq02.3 Ik00 Ik01.0 Qq01 xE0 "
     "xE1 Iq02 xE2 Wq10.0 Ik01.1 Qk00 xQ Wq10.1 R Wq10.2 Qq02 Wq10.3 M1q0 Wq11.0 Iq10 Wq11.1 Wq11.2 Qk01 "
     "Wq11.3 Ik02 E1q0 Wq12.0 M2q0 Qq10 Wq12.1 Iq11 Wq12.2 E2q0 Qk02 Wq12.3 Wq20.0 Ik10 M1k0 Wq20.1 Wq20.2 "
     "Qq11 Wq20.3 Iq12 E1k0 Wq21.0 M2k0 Qk10 Wq21.1 Ik11 Wq21.2 Wq21.3 Qq12 Wq22.0 Iq20 E2k0 M1q1 Wq22.1 "
@@ -36,7 +36,7 @@ ORDER = (
     "E1_0 P3 E1_1 M2_0 E1_2 E1_3 M2_1 E2_0 M2_2 E2_1 M2_3 E2_2 E2_3"
 )
 SEQ = "q00 q01 k00 q02 k01 q10 k02 q11 k10 q12 k11 q20 k12 q21 q22 k20 k21 k22"
-LOADS = "s q00 q01 k00 q02 x k01 q10 k02 q11 k10 c q12 k11 q20 k12 q21 q22 k20 k21 k22"
+LOADS = "s c q00 q01 k00 q02 x k01 q10 k02 q11 k10 q12 k11 q20 k12 q21 q22 k20 k21 k22"
 
 
 def tile_multiscaleretention_pa_kernel(tc, x, sin, cos, Wq_bytes, Wq_scale, Wk, out_0, out_1):
@@ -77,7 +77,10 @@ def tile_multiscaleretention_pa_kernel(tc, x, sin, cos, Wq_bytes, Wq_scale, Wk, 
 
         scl = keep.tile([P, PASSES, PACK], F32, name="scl")
         x_sb = keep.tile([P, E], BF16, name="x_sb")
-        cs = keep.tile([P, 2, DK], BF16, name="cs")
+        cs_row = keep.tile([P, 2 * DK], BF16, name="cs_row")
+        ones = keep.tile([P, P], BF16, name="ones")
+        nc.vector.memset(cs_row[:], 0.0)
+        nc.vector.memset(ones[:], 1.0)
 
         for s in LOADS.split():
             if s == "s":
@@ -85,8 +88,8 @@ def tile_multiscaleretention_pa_kernel(tc, x, sin, cos, Wq_bytes, Wq_scale, Wk, 
             elif s == "x":
                 nc.sync.dma_start(out=x_sb[:], in_=x2d)
             elif s == "c":
-                nc.sync.dma_start(out=cs[:, 0, :], in_=cos.rearrange("o d -> (o d)").partition_broadcast(P))
-                nc.sync.dma_start(out=cs[:, 1, :], in_=sin.rearrange("o d -> (o d)").partition_broadcast(P))
+                nc.scalar.dma_start(out=cs_row[0:1, 0:DK], in_=cos)
+                nc.scalar.dma_start(out=cs_row[0:1, DK : 2 * DK], in_=sin)
             else:
                 load((s[0], int(s[1]), int(s[2])))
 
@@ -107,12 +110,14 @@ def tile_multiscaleretention_pa_kernel(tc, x, sin, cos, Wq_bytes, Wq_scale, Wk, 
         x_codes = keep.tile([P, PASSES, B], U32, name="x_codes", align_bytes=64)
         x_scales = keep.tile([P, PASSES, B], U8, name="x_scales", align_bytes=64)
 
+        spread = {}
+
         def build_rot():
             prod = keep.tile([P, 2, P], F32, name="prod")
             nc.vector.tensor_tensor(
                 out=prod[:].rearrange("p s (h d) -> p s h d", h=2),
                 in0=idsw[:].rearrange("p s (h d) -> p s h d", h=2),
-                in1=cs[:].unsqueeze(2).to_broadcast([P, 2, 2, DK]),
+                in1=spread["cs"][:].rearrange("p (s d) -> p s d", s=2).unsqueeze(2).to_broadcast([P, 2, 2, DK]),
                 op=ALU.mult,
             )
             nc.vector.tensor_tensor(out=rot[:], in0=prod[:, 0, :], in1=prod[:, 1, :], op=ALU.add)
@@ -223,6 +228,10 @@ def tile_multiscaleretention_pa_kernel(tc, x, sin, cos, Wq_bytes, Wq_scale, Wk, 
             elif tok == "xQ":
                 for g in range(PASSES):
                     nc.vector.quantize_mx(out=x_codes[:, g, :].bitcast(FP8X4), scales=x_scales[:, g, :], in_=x_grp[:, g, :])
+            elif tok == "B":
+                cs_all = pst.tile([P, 2 * DK], F32, name="cs_all", tag="bank")
+                nc.tensor.matmul(out=cs_all[:], lhsT=ones[:], rhs=cs_row[:], start=True, stop=True)
+                spread["cs"] = cs_all
             elif tok == "R":
                 build_rot()
             elif tok.startswith("Mpre"):

@@ -31,8 +31,8 @@ ORDER = (
     "xE1 Iq02 xE2 Wq10.0 Ik01.1 Qk00 xQ Wq10.1 R Wq10.2 Qq02 Wq10.3 M1q0 Wq11.0 Iq10 Wq11.1 Wq11.2 Qk01 "
     "Wq11.3 Ik02 E1q0 Wq12.0 M2q0 Qq10 Wq12.1 Iq11 Wq12.2 E2q0 Qk02 Wq12.3 Wq20.0 Ik10 M1k0 Wq20.1 Wq20.2 "
     "Qq11 Wq20.3 Iq12 E1k0 Wq21.0 M2k0 Qk10 Wq21.1 Ik11 Wq21.2 Wq21.3 Qq12 Wq22.0 Iq20 E2k0 M1q1 Wq22.1 "
-    "Wq22.2 Qk11 E1q1 Ik12 Wq22.3 M2q1 Iq22.0 Qq20 Iq21 E2q1 Iq22.1 Qk12 Qq21 M1k1 Ik20.0 Qq22 Ik21 "
-    "Ik20.1 M1q2 E1k1 Qk20 E1q2 M2k1 I0 Qk21 I1 M2q2 E2k1 Q0 I2 Q1 Mpre0 I3 E2q2 Mpre1 Q2 P0 Q3 P1 P2 "
+    "Wq22.2 Qk11 E1q1 Ik12 Wq22.3 M2q1 Iq22.0 Qq20 Iq21 E2q1 Iq22.1 Qk12 Qq21 M1k1 Ik20 Qq22 Ik21 "
+    "M1q2 E1k1 Qk20 E1q2 M2k1 I0 Qk21 I1 M2q2 E2k1 Q0 I2 Q1 Mpre0 I3 E2q2 Mpre1 Q2 P0 Q3 P1 P2 "
     "E1_0 P3 E1_1 M2_0 E1_2 E1_3 M2_1 E2_0 M2_2 E2_1 M2_3 E2_2 E2_3"
 )
 SEQ = "q00 q01 k00 q02 k01 q10 k02 q11 k10 q12 k11 q20 k12 q21 q22 k20 k21 k22"

@@ -36,7 +36,7 @@ ORDER = (
     "E1_0 P3 E1_1 M2_0 E1_2 E1_3 M2_1 E2_0 M2_2 E2_1 M2_3 E2_2 E2_3"
 )
 SEQ = "q00 q01 k00 q02 k01 q10 k02 q11 k10 q12 k11 q20 k12 q21 q22 k20 k21 k22"
-LOADS = "s c q00 q01 k00 q02 x k01 q10 k02 q11 k10 q12 k11 q20 k12 q21 q22 k20 k21 k22"
+LOADS = "c s q00 q01 k00 q02 x k01 q10 k02 q11 k10 q12 k11 q20 k12 q21 q22 k20 k21 k22"
 
 
 def tile_multiscaleretention_pa_kernel(tc, x, sin, cos, Wq_bytes, Wq_scale, Wk, out_0, out_1):
@@ -84,12 +84,12 @@ def tile_multiscaleretention_pa_kernel(tc, x, sin, cos, Wq_bytes, Wq_scale, Wk, 
 
         for s in LOADS.split():
             if s == "s":
-                nc.scalar.dma_start(out=scl[:], in_=Wq_scale.rearrange("(g p t) o -> p g (t o)", p=P, t=PACK))
+                nc.sync.dma_start(out=scl[:], in_=Wq_scale.rearrange("(g p t) o -> p g (t o)", p=P, t=PACK))
             elif s == "x":
                 nc.sync.dma_start(out=x_sb[:], in_=x2d)
             elif s == "c":
-                nc.scalar.dma_start(out=cs_row[0:1, 0:DK], in_=cos)
-                nc.scalar.dma_start(out=cs_row[0:1, DK : 2 * DK], in_=sin)
+                nc.sync.dma_start(out=cs_row[0:1, 0:DK], in_=cos)
+                nc.sync.dma_start(out=cs_row[0:1, DK : 2 * DK], in_=sin)
             else:
                 load((s[0], int(s[1]), int(s[2])))
 

@@ -31,7 +31,7 @@ ORDER = (
     "xE1 Iq02 xE2 Wq10.0 Ik01.1 Qk00 xQ Wq10.1 R Wq10.2 Qq02 Wq10.3 M1q0 Wq11.0 Iq10 Wq11.1 Wq11.2 Qk01 "
     "Wq11.3 Ik02 E1q0 Wq12.0 M2q0 Qq10 Wq12.1 Iq11 Wq12.2 E2q0 Qk02 Wq12.3 Wq20.0 Ik10 M1k0 Wq20.1 Wq20.2 "
     "Qq11 Wq20.3 Iq12 E1k0 Wq21.0 M2k0 Qk10 Wq21.1 Ik11 Wq21.2 Wq21.3 Qq12 Wq22.0 Iq20 E2k0 M1q1 Wq22.1 "
-    "Wq22.2 Qk11 E1q1 Ik12 Wq22.3 M2q1 Iq22.0 Qq20 Iq21 E2q1 Iq22.1 Qk12 Qq21 M1k1 Ik20 Qq22 Ik21 "
+    "Wq22.2 Qk11 E1q1 Ik12 Wq22.3 M2q1 Iq22.0 Qq20 Iq21 E2q1 Iq22.1 Qk12 Qq21 M1k1 Dk10 Dk11 Ik20 Qq22 Ik21 "
     "M1q2 E1k1 Qk20 E1q2 M2k1 I0 Qk21 I1 M2q2 E2k1 Q0 I2 Q1 Mpre0 I3 E2q2 Mpre1 Q2 P0 Q3 P1 P2 "
     "E1_0 P3 E1_1 M2_0 E1_2 E1_3 M2_1 E2_0 M2_2 E2_1 M2_3 E2_2 E2_3"
 )
@@ -228,6 +228,21 @@ def tile_multiscaleretention_pa_kernel(tc, x, sin, cos, Wq_bytes, Wq_scale, Wk, 
             elif tok == "xQ":
                 for g in range(PASSES):
                     nc.vector.quantize_mx(out=x_codes[:, g, :].bitcast(FP8X4), scales=x_scales[:, g, :], in_=x_grp[:, g, :])
+            elif tok.startswith("D"):
+                m, c, g = unit(tok[1:4])
+                if "scratch" not in spread:
+                    scratch = pst.tile([P, CHUNK], F32, name="scratch", tag="bank")
+                    spread["scratch"] = scratch
+                for rep_no in range(2):
+                    nc.tensor.matmul_mx(
+                        out=spread["scratch"][:],
+                        lhsT=x_codes[:, g, :].bitcast(FP8X4),
+                        lhsT_scale=x_scales[:, g, :],
+                        rhs=codes[(m, c)][:, g, :].bitcast(FP8X4),
+                        rhs_scale=scales[(m, c)][:, g, :],
+                        start=True,
+                        stop=True,
+                    )
             elif tok == "B":
                 cs_all = pst.tile([P, 2 * DK], F32, name="cs_all", tag="bank")
                 nc.tensor.matmul(out=cs_all[:], lhsT=ones[:], rhs=cs_row[:], start=True, stop=True)

@@ -24,18 +24,23 @@ CHUNK = 512
 CHUNKS = HK // CHUNK
 TILES = CHUNK // P
 
+X_STATIONARY = (2, 3)
+
 FLOPS = 2 * 2 * B * E * HK
 
-ORDER = (
-    "Wq00 Wq01.0 Wq01.1 Iq00 Wq01.2 Wq01.3 Wq02.0 Iq01 Wq02.1 xT B Wq02.2 Qq00 Wq02.3 Ik00 Ik01.0 Qq01 xE0 "
-    "xE1 Iq02 xE2 Wq10.0 Ik01.1 Qk00 xQ Wq10.1 R Wq10.2 Qq02 Wq10.3 M1q0 Wq11.0 Iq10 Wq11.1 Wq11.2 Qk01 "
-    "Wq11.3 Ik02 E1q0 Wq12.0 M2q0 Qq10 Wq12.1 Iq11 Wq12.2 E2q0 Qk02 Wq12.3 Wq20.0 Ik10 M1k0 Wq20.1 Wq20.2 "
-    "Qq11 Wq20.3 Iq12 E1k0 Wq21.0 M2k0 Qk10 Wq21.1 Ik11 Wq21.2 Wq21.3 Qq12 Wq22.0 Iq20 E2k0 M1q1 Wq22.1 "
-    "Wq22.2 Qk11 E1q1 Ik12 Wq22.3 M2q1 Iq22.0 Qq20 Iq21 E2q1 Iq22.1 Qk12 Qq21 M1k1 Dk10 Dk11 Ik20 Qq22 Ik21 "
-    "M1q2 E1k1 Qk20 E1q2 M2k1 I0 Qk21 I1 M2q2 E2k1 Q0 I2 Q1 Mpre0 I3 E2q2 Mpre1 Q2 P0 Q3 P1 P2 "
-    "E1_0 P3 E1_1 M2_0 E1_2 E1_3 M2_1 E2_0 M2_2 E2_1 M2_3 E2_2 E2_3"
+VECTOR = (
+    "Wq00 Iq00 Ik00 Qq00 Iq01 Qk00 Iq02 Qq01 Ik01 xQ Qq02 R Ik02 Qk01 Iq10 Qk02 Iq11 Qq10 Ik10 Qq11 Iq12 "
+    "Qk10 Ik11 Qq12 Iq20 Qk11 Ik12 Qq20 Iq21 Qk12 Iq22v0 Qq21 I0 Qq22 I1 Qk20 I2 I3 Q0 Qk21 Q1 Q2 Q3 F"
 )
-SEQ = "q00 q01 k00 q02 k01 q10 k02 q11 k10 q12 k11 q20 k12 q21 q22 k20 k21 k22"
+SCALAR = (
+    "Wq01.0 Wq01.1 Wq01.2 Wq01.3 Wq02.0 Wq02.1 Wq02.2 Wq02.3 xE0 xE1 xE2 C Wq10.0 Wq10.1 Wq10.2 Wq10.3 "
+    "Wq11.0 Wq11.1 Wq11.2 Wq11.3 E1q0 Wq12.0 Wq12.1 Wq12.2 Wq12.3 Wq20.0 Wq20.1 E1k0 E2q0 Wq20.2 Wq20.3 "
+    "Wq21.0 E2k0 Wq21.1 Wq21.2 Wq21.3 Ik20.0 Wq22.0 Wq22.1 E1q1 Wq22.2 Wq22.3 Iq22.1 Ik20.1 E2q1 Ik21.0 "
+    "E1k1 Ik21.1 E1q2 E2k1 E2q2 E1_0 E1_1 E2_0 E2_1"
+)
+TENSOR = (
+    "B xT M1q0 M2q0 M1k0 M2k0 M1q1 M2q1 M1k1 M1q2 M2k1 Mpre0 M2q2 Mpre1 P0 P1 P2 P3 M2_0 M2_1"
+)
 LOADS = "c s q00 q01 k00 q02 x k01 q10 k02 q11 k10 q12 k11 q20 k12 q21 q22 k20 k21 k22"
 
 
@@ -50,12 +55,11 @@ def tile_multiscaleretention_pa_kernel(tc, x, sin, cos, Wq_bytes, Wq_scale, Wk, 
     wq_view = Wq_bytes.rearrange("(g p t) n -> g p t n", p=P, t=PACK)
 
     chunks = [(m, c) for c in range(CHUNKS) for m in ("q", "k")]
-    units = [(s[0], int(s[1]), int(s[2])) for s in SEQ.split()]
 
     with ExitStack() as ctx:
         keep = ctx.enter_context(tc.tile_pool(name="keep", bufs=1))
         wide_pool = ctx.enter_context(tc.tile_pool(name="wide", bufs=9))
-        grp_pool = ctx.enter_context(tc.tile_pool(name="grp", bufs=6))
+        grp_pool = ctx.enter_context(tc.tile_pool(name="grp", bufs=10))
         qt_pool = ctx.enter_context(tc.tile_pool(name="qt", bufs=3))
         res_pool = ctx.enter_context(tc.tile_pool(name="res", bufs=9))
         pst = ctx.enter_context(tc.psum_pool(name="pst", bufs=4))
@@ -82,14 +86,15 @@ def tile_multiscaleretention_pa_kernel(tc, x, sin, cos, Wq_bytes, Wq_scale, Wk, 
         nc.vector.memset(cs_row[:], 0.0)
         nc.vector.memset(ones[:], 1.0)
 
+        small = nc.sync
         for s in LOADS.split():
             if s == "s":
                 nc.sync.dma_start(out=scl[:], in_=Wq_scale.rearrange("(g p t) o -> p g (t o)", p=P, t=PACK))
             elif s == "x":
                 nc.sync.dma_start(out=x_sb[:], in_=x2d)
             elif s == "c":
-                nc.sync.dma_start(out=cs_row[0:1, 0:DK], in_=cos)
-                nc.sync.dma_start(out=cs_row[0:1, DK : 2 * DK], in_=sin)
+                small.dma_start(out=cs_row[0:1, 0:DK], in_=cos)
+                small.dma_start(out=cs_row[0:1, DK : 2 * DK], in_=sin)
             else:
                 load((s[0], int(s[1]), int(s[2])))
 
@@ -98,8 +103,11 @@ def tile_multiscaleretention_pa_kernel(tc, x, sin, cos, Wq_bytes, Wq_scale, Wk, 
         ident = idsw[:, 0, :]
         id_pairs = idsw[:, 0, :].rearrange("p (i two) -> p i two", two=2)
         sw_pairs = idsw[:, 1, :].rearrange("p (i two) -> p i two", two=2)
-        nc.gpsimd.tensor_scalar(out=sw_pairs[:, :, 0], in0=id_pairs[:, :, 1], scalar1=-1.0, scalar2=None, op0=ALU.mult)
+        nc.gpsimd.tensor_copy(out=sw_pairs[:, :, 0], in_=id_pairs[:, :, 1])
         nc.gpsimd.tensor_copy(out=sw_pairs[:, :, 1], in_=id_pairs[:, :, 0])
+        nc.gpsimd.tensor_scalar(
+            out=cs_row[:, DK : 2 * DK : 2], in0=cs_row[:, DK : 2 * DK : 2], scalar1=-1.0, scalar2=None, op0=ALU.mult
+        )
 
         warm = keep.tile([P, 2], F32, name="warm")
         nc.vector.memset(warm[:, 0:1], 0.0)
@@ -174,6 +182,17 @@ def tile_multiscaleretention_pa_kernel(tc, x, sin, cos, Wq_bytes, Wq_scale, Wk, 
         def passes(ch, acc_cols, j, gs):
             cols = slice(j * P, (j + 1) * P)
             for g in gs:
+                if ch == last_ch and j in X_STATIONARY:
+                    nc.tensor.matmul_mx(
+                        out=acc_cols,
+                        lhsT=x_codes[:, g, :].bitcast(FP8X4),
+                        lhsT_scale=x_scales[:, g, :],
+                        rhs=codes[ch][:, g, cols].bitcast(FP8X4),
+                        rhs_scale=scales[ch][:, g, cols],
+                        start=(g == 0),
+                        stop=(g == PASSES - 1),
+                    )
+                    continue
                 nc.tensor.matmul_mx(
                     out=acc_cols,
                     lhsT=codes[ch][:, g, cols].bitcast(FP8X4),
@@ -207,7 +226,46 @@ def tile_multiscaleretention_pa_kernel(tc, x, sin, cos, Wq_bytes, Wq_scale, Wk, 
             lo = c * CHUNK + first_tile * P
             nc.sync.dma_start(out=outs[m][:, lo : lo + width], in_=res[:, :width])
 
-        last = units[len(units) - 1]
+        cs = keep.tile([P, 2, DK], F32, name="cs")
+
+        def build_cs():
+            nc.scalar.copy(out=cs[:].rearrange("p s d -> p (s d)"), in_=spread["cs"][:])
+
+        def rotate_last(js):
+            m, c = last_ch
+            parts = {}
+            for j in js:
+                straight = keep.tile([P, P], F32, name="straight%d" % j)
+                crossed = keep.tile([P, P], F32, name="crossed%d" % j)
+                parts[j] = (straight, crossed)
+
+            def products(j):
+                nc.vector.tensor_tensor(
+                    out=parts[j][0][:].rearrange("p (h d) -> p h d", h=2),
+                    in0=acc[j][:].rearrange("p (h d) -> p h d", h=2),
+                    in1=cs[:, 0, :].unsqueeze(1).to_broadcast([P, 2, DK]),
+                    op=ALU.mult,
+                )
+                nc.vector.tensor_tensor(
+                    out=parts[j][1][:].rearrange("p (h i two) -> p h i two", h=2, two=2),
+                    in0=acc[j][:].rearrange("p (h i two) -> p h i two", h=2, two=2)[:, :, :, ::-1],
+                    in1=cs[:, 1, :].rearrange("p (i two) -> p i two", two=2).unsqueeze(1).to_broadcast([P, 2, DK // 2, 2]),
+                    op=ALU.mult,
+                )
+
+            def finish(j):
+                res = res_pool.tile([P, CHUNK], F32, name="res")
+                nc.vector.tensor_tensor(out=res[:, :P], in0=parts[j][0][:], in1=parts[j][1][:], op=ALU.add)
+                lo = c * CHUNK + j * P
+                nc.sync.dma_start(out=outs[m][:, lo : lo + P], in_=res[:, :P])
+
+            products(js[0])
+            for n in range(1, len(js)):
+                products(js[n])
+                finish(js[n - 1])
+            finish(js[len(js) - 1])
+
+        last = ("k", CHUNKS - 1, PASSES - 1)
         last_ch = (last[0], last[1])
         xts = {}
         words = x_sb[:].bitcast(F32)
@@ -228,27 +286,16 @@ def tile_multiscaleretention_pa_kernel(tc, x, sin, cos, Wq_bytes, Wq_scale, Wk, 
             elif tok == "xQ":
                 for g in range(PASSES):
                     nc.vector.quantize_mx(out=x_codes[:, g, :].bitcast(FP8X4), scales=x_scales[:, g, :], in_=x_grp[:, g, :])
-            elif tok.startswith("D"):
-                m, c, g = unit(tok[1:4])
-                if "scratch" not in spread:
-                    scratch = pst.tile([P, CHUNK], F32, name="scratch", tag="bank")
-                    spread["scratch"] = scratch
-                for rep_no in range(2):
-                    nc.tensor.matmul_mx(
-                        out=spread["scratch"][:],
-                        lhsT=x_codes[:, g, :].bitcast(FP8X4),
-                        lhsT_scale=x_scales[:, g, :],
-                        rhs=codes[(m, c)][:, g, :].bitcast(FP8X4),
-                        rhs_scale=scales[(m, c)][:, g, :],
-                        start=True,
-                        stop=True,
-                    )
             elif tok == "B":
                 cs_all = pst.tile([P, 2 * DK], F32, name="cs_all", tag="bank")
                 nc.tensor.matmul(out=cs_all[:], lhsT=ones[:], rhs=cs_row[:], start=True, stop=True)
                 spread["cs"] = cs_all
             elif tok == "R":
                 build_rot()
+            elif tok == "C":
+                build_cs()
+            elif tok == "F":
+                rotate_last(X_STATIONARY)
             elif tok.startswith("Mpre"):
                 g = int(tok[4])
                 for j in range(TILES):
@@ -267,7 +314,7 @@ def tile_multiscaleretention_pa_kernel(tc, x, sin, cos, Wq_bytes, Wq_scale, Wk, 
             elif tok.startswith("M2_"):
                 rotate(int(tok[3]), 1)
             elif tok.startswith("E2_"):
-                store(int(tok[3]), last_ch, int(tok[3]), 1, True)
+                store(int(tok[3]), last_ch, int(tok[3]), 1, False)
             elif tok.startswith("E1"):
                 copy_out((tok[2], int(tok[3])), CHUNK)
             elif tok.startswith("M2"):
@@ -288,6 +335,9 @@ def tile_multiscaleretention_pa_kernel(tc, x, sin, cos, Wq_bytes, Wq_scale, Wk, 
                 quantize(last, int(tok[1]) * P, (int(tok[1]) + 1) * P)
             elif tok.startswith("I") and len(tok) == 4:
                 interleave(unit(tok[1:4]), 0, CHUNK, True)
+            elif tok.startswith("I") and tok[4] == "v":
+                h = int(tok[5])
+                interleave(unit(tok[1:4]), h * CHUNK // 2, (h + 1) * CHUNK // 2, True)
             elif tok.startswith("I"):
                 h = int(tok[5])
                 interleave(unit(tok[1:4]), h * CHUNK // 2, (h + 1) * CHUNK // 2, False)
@@ -296,6 +346,53 @@ def tile_multiscaleretention_pa_kernel(tc, x, sin, cos, Wq_bytes, Wq_scale, Wk, 
             else:
                 raise ValueError(tok)
 
+        queues = [VECTOR.split(), SCALAR.split(), TENSOR.split()]
+        names = [q for queue in queues for q in queue]
+        written = set()
+
+        def needs(tok):
+            u = tok[1:4]
+            if tok.startswith("xE"):
+                return ["xT"]
+            if tok == "xQ":
+                return ["xE%d" % g for g in range(PASSES)]
+            if tok in ("R", "C"):
+                return ["B"]
+            if tok.startswith("Iq"):
+                return [n for n in names if n.startswith("W" + u)]
+            if tok.startswith("Qq") or tok.startswith("Qk"):
+                return [n for n in names if n.startswith("I" + u)]
+            if tok.startswith("Q"):
+                return ["I" + tok[1]]
+            if tok.startswith("Mpre"):
+                return ["xQ", "Q%s%d%s" % (last_ch[0], last_ch[1], tok[4])]
+            if tok.startswith("M2_"):
+                return ["E1_" + tok[3], "R"]
+            if tok.startswith("P"):
+                return ["Mpre1", "Q" + tok[1]]
+            if tok.startswith("E1_"):
+                return ["P" + tok[3]]
+            if tok.startswith("E2_"):
+                return ["M2_" + tok[3]]
+            if tok.startswith("M1"):
+                older = chunks.index((tok[2], int(tok[3]))) - 2
+                return ["xQ"] + ["Q%s%d" % (tok[2:4], g) for g in range(PASSES)] + (["E1%s%d" % chunks[older]] if older >= 0 else [])
+            if tok.startswith("M2"):
+                older = chunks.index((tok[2], int(tok[3]))) - 2
+                return ["E1" + tok[2:4], "R"] + (["E2%s%d" % chunks[older]] if older >= 0 else [])
+            if tok.startswith("E"):
+                return ["M" + tok[1:4]]
+            if tok == "F":
+                return ["C"] + ["P%d" % j for j in X_STATIONARY]
+            return []
+
         with tc.manual_schedule():
-            for tok in ORDER.split():
-                run(tok)
+            at = [0, 0, 0]
+            while len(written) < len(names):
+                before = len(written)
+                for e, queue in enumerate(queues):
+                    if at[e] < len(queue) and all(n in written for n in needs(queue[at[e]])):
+                        run(queue[at[e]])
+                        written.add(queue[at[e]])
+                        at[e] = at[e] + 1
+                assert len(written) > before

@@ -24,22 +24,23 @@ CHUNK = 512
 CHUNKS = HK // CHUNK
 TILES = CHUNK // P
 
-X_STATIONARY = (2, 3)
+HALF = CHUNK // 2
 
 FLOPS = 2 * 2 * B * E * HK
 
 VECTOR = (
-    "Wq00 Iq00 Ik00 Qq00 Iq01 Qk00 Iq02 Qq01 Ik01 xQ Qq02 R Ik02 Qk01 Iq10 Qk02 Iq11 Qq10 Ik10 Qq11 Iq12 "
-    "Qk10 Ik11 Qq12 Iq20 Qk11 Ik12 Qq20 Iq21 Qk12 Iq22v0 Qq21 I0 Qq22 I1 Qk20 I2 I3 Q0 Qk21 Q1 Q2 Q3 F"
+    "Wq00.0 Wq00.1 Wq00.2 Iq00 Ik00 Qq00 Iq01 Qk00 Iq02 Qq01 Ik01 xQ Qq02 R Ik02 Qk01 Iq10 Qk02 Iq11 Qq10 "
+    "Ik10v0 Qq11 Iq12 Qk10 Ik11 Qq12 Iq20 Qk11 Ik12 Qq20 Iq21 Qk12 Iq22v0 Qq21 Ia Qq22 Ik21v0 Ib Qk20 Qa "
+    "Qk21 Qb Fa Fb"
 )
 SCALAR = (
-    "Wq01.0 Wq01.1 Wq01.2 Wq01.3 Wq02.0 Wq02.1 Wq02.2 Wq02.3 xE0 xE1 xE2 C Wq10.0 Wq10.1 Wq10.2 Wq10.3 "
-    "Wq11.0 Wq11.1 Wq11.2 Wq11.3 E1q0 Wq12.0 Wq12.1 Wq12.2 Wq12.3 Wq20.0 Wq20.1 E1k0 E2q0 Wq20.2 Wq20.3 "
-    "Wq21.0 E2k0 Wq21.1 Wq21.2 Wq21.3 Ik20.0 Wq22.0 Wq22.1 E1q1 Wq22.2 Wq22.3 Iq22.1 Ik20.1 E2q1 Ik21.0 "
-    "E1k1 Ik21.1 E1q2 E2k1 E2q2 E1_0 E1_1 E2_0 E2_1"
+    "Wq00.3 Wq01.0 Wq01.1 Wq01.2 Wq01.3 Wq02.0 Wq02.1 Wq02.2 Wq02.3 xE0 xE1 xE2 C Wq10.0 Wq10.1 Wq10.2 "
+    "Wq10.3 Wq11.0 Wq11.1 Wq11.2 Wq11.3 Ik10.1 E1q0 Wq12.0 Wq12.1 Wq12.2 Wq12.3 Wq20.0 Wq20.1 E1k0 E2q0 "
+    "Wq20.2 Wq20.3 Wq21.0 E2k0 Wq21.1 Wq21.2 Wq21.3 Wq22.0 Wq22.1 Wq22.2 E1q1 Wq22.3 Iq22.1 Ik20.0 E2q1 "
+    "Ik20.1 E1k1 Ik21.1 E1q2 E2k1 E2q2"
 )
 TENSOR = (
-    "B xT M1q0 M2q0 M1k0 M2k0 M1q1 M2q1 M1k1 M1q2 M2k1 Mpre0 M2q2 Mpre1 P0 P1 P2 P3 M2_0 M2_1"
+    "B xT M1q0 M2q0 M1k0 M2k0 M1q1 M2q1 M1k1 M1q2 M2k1 Mpre0 Mpre1 Pa Pb M2q2"
 )
 LOADS = "c s q00 q01 k00 q02 x k01 q10 k02 q11 k10 q12 k11 q20 k12 q21 q22 k20 k21 k22"
 
@@ -179,91 +180,82 @@ def tile_multiscaleretention_pa_kernel(tc, x, sin, cos, Wq_bytes, Wq_scale, Wk, 
                 in_=grp[u][:, lo:hi, :].rearrange("p n t -> p (n t)"),
             )
 
-        def passes(ch, acc_cols, j, gs):
-            cols = slice(j * P, (j + 1) * P)
-            for g in gs:
-                if ch == last_ch and j in X_STATIONARY:
+        def passes(ch):
+            a = ps1.tile([P, CHUNK], F32, name="acc")
+            acc[ch] = a
+            for j in range(TILES):
+                cols = slice(j * P, (j + 1) * P)
+                for g in range(PASSES):
                     nc.tensor.matmul_mx(
-                        out=acc_cols,
-                        lhsT=x_codes[:, g, :].bitcast(FP8X4),
-                        lhsT_scale=x_scales[:, g, :],
-                        rhs=codes[ch][:, g, cols].bitcast(FP8X4),
-                        rhs_scale=scales[ch][:, g, cols],
+                        out=a[:, cols],
+                        lhsT=codes[ch][:, g, cols].bitcast(FP8X4),
+                        lhsT_scale=scales[ch][:, g, cols],
+                        rhs=x_codes[:, g, :].bitcast(FP8X4),
+                        rhs_scale=x_scales[:, g, :],
                         start=(g == 0),
                         stop=(g == PASSES - 1),
                     )
-                    continue
-                nc.tensor.matmul_mx(
-                    out=acc_cols,
-                    lhsT=codes[ch][:, g, cols].bitcast(FP8X4),
-                    lhsT_scale=scales[ch][:, g, cols],
-                    rhs=x_codes[:, g, :].bitcast(FP8X4),
-                    rhs_scale=x_scales[:, g, :],
-                    start=(g == 0),
-                    stop=(g == PASSES - 1),
-                )
 
-        def copy_out(key, width):
+        def x_stationary(half, g):
+            if half not in acc:
+                acc_t = pst.tile([P, HALF], F32, name="acc_t", tag="bank")
+                acc[half] = acc_t
+            cols = slice(half * HALF, (half + 1) * HALF)
+            nc.tensor.matmul_mx(
+                out=acc[half][:],
+                lhsT=x_codes[:, g, :].bitcast(FP8X4),
+                lhsT_scale=x_scales[:, g, :],
+                rhs=codes[last_ch][:, g, cols].bitcast(FP8X4),
+                rhs_scale=scales[last_ch][:, g, cols],
+                start=(g == 0),
+                stop=(g == PASSES - 1),
+            )
+
+        def copy_out(ch):
             qt = qt_pool.tile([P, CHUNK], F32, name="qt")
-            nc.scalar.copy(out=qt[:, :width], in_=acc[key][:, :width])
-            qts[key] = qt
+            nc.scalar.copy(out=qt[:], in_=acc[ch][:])
+            qts[ch] = qt
 
-        def rotate(key, n_tiles):
+        def rotate(ch):
             tu = ps2.tile([P, CHUNK], F32, name="turned")
-            for j in range(n_tiles):
+            for j in range(TILES):
                 cols = slice(j * P, (j + 1) * P)
-                nc.tensor.matmul(out=tu[:, cols], lhsT=qts[key][:, cols], rhs=rot[:], start=True, stop=True)
-            turned[key] = tu
+                nc.tensor.matmul(out=tu[:, cols], lhsT=qts[ch][:, cols], rhs=rot[:], start=True, stop=True)
+            turned[ch] = tu
 
-        def store(key, ch, first_tile, n_tiles, on_vector):
+        def store(ch):
             m, c = ch
-            width = n_tiles * P
             res = res_pool.tile([P, CHUNK], F32, name="res")
-            if on_vector:
-                nc.vector.tensor_copy(out=res[:, :width], in_=turned[key][:, :width])
-            else:
-                nc.scalar.copy(out=res[:, :width], in_=turned[key][:, :width])
-            lo = c * CHUNK + first_tile * P
-            nc.sync.dma_start(out=outs[m][:, lo : lo + width], in_=res[:, :width])
+            nc.scalar.copy(out=res[:], in_=turned[ch][:])
+            nc.sync.dma_start(out=outs[m][:, c * CHUNK : (c + 1) * CHUNK], in_=res[:])
 
         cs = keep.tile([P, 2, DK], F32, name="cs")
 
         def build_cs():
             nc.scalar.copy(out=cs[:].rearrange("p s d -> p (s d)"), in_=spread["cs"][:])
 
-        def rotate_last(js):
+        def rotate_last(half):
             m, c = last_ch
-            parts = {}
-            for j in js:
-                straight = keep.tile([P, P], F32, name="straight%d" % j)
-                crossed = keep.tile([P, P], F32, name="crossed%d" % j)
-                parts[j] = (straight, crossed)
-
-            def products(j):
-                nc.vector.tensor_tensor(
-                    out=parts[j][0][:].rearrange("p (h d) -> p h d", h=2),
-                    in0=acc[j][:].rearrange("p (h d) -> p h d", h=2),
-                    in1=cs[:, 0, :].unsqueeze(1).to_broadcast([P, 2, DK]),
-                    op=ALU.mult,
-                )
-                nc.vector.tensor_tensor(
-                    out=parts[j][1][:].rearrange("p (h i two) -> p h i two", h=2, two=2),
-                    in0=acc[j][:].rearrange("p (h i two) -> p h i two", h=2, two=2)[:, :, :, ::-1],
-                    in1=cs[:, 1, :].rearrange("p (i two) -> p i two", two=2).unsqueeze(1).to_broadcast([P, 2, DK // 2, 2]),
-                    op=ALU.mult,
-                )
-
-            def finish(j):
-                res = res_pool.tile([P, CHUNK], F32, name="res")
-                nc.vector.tensor_tensor(out=res[:, :P], in0=parts[j][0][:], in1=parts[j][1][:], op=ALU.add)
-                lo = c * CHUNK + j * P
-                nc.sync.dma_start(out=outs[m][:, lo : lo + P], in_=res[:, :P])
-
-            products(js[0])
-            for n in range(1, len(js)):
-                products(js[n])
-                finish(js[n - 1])
-            finish(js[len(js) - 1])
+            heads = HALF // DK
+            straight = keep.tile([P, HALF], F32, name="straight%d" % half)
+            crossed = keep.tile([P, HALF], F32, name="crossed%d" % half)
+            res = res_pool.tile([P, CHUNK], F32, name="res")
+            nc.vector.tensor_tensor(
+                out=straight[:].rearrange("p (h d) -> p h d", h=heads),
+                in0=acc[half][:].rearrange("p (h d) -> p h d", h=heads),
+                in1=cs[:, 0, :].unsqueeze(1).to_broadcast([P, heads, DK]),
+                op=ALU.mult,
+            )
+            nc.vector.tensor_tensor(
+                out=crossed[:].rearrange("p (h i two) -> p h i two", h=heads, two=2),
+                in0=acc[half][:].rearrange("p (h i two) -> p h i two", h=heads, two=2)[:, :, :, ::-1],
+                in1=cs[:, 1, :].rearrange("p (i two) -> p i two", two=2).unsqueeze(1).to_broadcast([P, heads, DK // 2, 2]),
+                op=ALU.mult,
+            )
+            adder = nc.gpsimd if half == 0 else nc.vector
+            adder.tensor_tensor(out=res[:, :HALF], in0=straight[:], in1=crossed[:], op=ALU.add)
+            lo = c * CHUNK + half * HALF
+            nc.sync.dma_start(out=outs[m][:, lo : lo + HALF], in_=res[:, :HALF])
 
         last = ("k", CHUNKS - 1, PASSES - 1)
         last_ch = (last[0], last[1])
@@ -294,45 +286,29 @@ def tile_multiscaleretention_pa_kernel(tc, x, sin, cos, Wq_bytes, Wq_scale, Wk, 
                 build_rot()
             elif tok == "C":
                 build_cs()
-            elif tok == "F":
-                rotate_last(X_STATIONARY)
+            elif tok in ("Fa", "Fb"):
+                rotate_last("ab".index(tok[1]))
             elif tok.startswith("Mpre"):
-                g = int(tok[4])
-                for j in range(TILES):
-                    if g == 0:
-                        acc_t = pst.tile([P, P], F32, name="acc_t", tag="bank")
-                        acc[j] = acc_t
-                    passes(last_ch, acc[j][:], j, [g])
+                for half in range(2):
+                    x_stationary(half, int(tok[4]))
+            elif tok in ("Pa", "Pb"):
+                x_stationary("ab".index(tok[1]), PASSES - 1)
             elif tok.startswith("M1"):
-                ch = (tok[2], int(tok[3]))
-                a = ps1.tile([P, CHUNK], F32, name="acc")
-                acc[ch] = a
-                for j in range(TILES):
-                    passes(ch, a[:, j * P : (j + 1) * P], j, range(PASSES))
-            elif tok.startswith("E1_"):
-                copy_out(int(tok[3]), P)
-            elif tok.startswith("M2_"):
-                rotate(int(tok[3]), 1)
-            elif tok.startswith("E2_"):
-                store(int(tok[3]), last_ch, int(tok[3]), 1, False)
+                passes((tok[2], int(tok[3])))
             elif tok.startswith("E1"):
-                copy_out((tok[2], int(tok[3])), CHUNK)
+                copy_out((tok[2], int(tok[3])))
             elif tok.startswith("M2"):
-                rotate((tok[2], int(tok[3])), TILES)
+                rotate((tok[2], int(tok[3])))
             elif tok.startswith("E2"):
-                store((tok[2], int(tok[3])), (tok[2], int(tok[3])), 0, TILES, False)
+                store((tok[2], int(tok[3])))
             elif tok.startswith("W"):
-                if len(tok) == 4:
-                    for t in range(PACK):
-                        widen(unit(tok[1:4]), t, True)
-                else:
-                    widen(unit(tok[1:4]), int(tok[5]), False)
-            elif tok.startswith("P"):
-                passes(last_ch, acc[int(tok[1])][:], int(tok[1]), [PASSES - 1])
-            elif tok.startswith("I") and len(tok) == 2:
-                interleave(last, int(tok[1]) * P, (int(tok[1]) + 1) * P, True)
-            elif tok.startswith("Q") and len(tok) == 2:
-                quantize(last, int(tok[1]) * P, (int(tok[1]) + 1) * P)
+                widen(unit(tok[1:4]), int(tok[5]), tok in VECTOR.split())
+            elif tok in ("Ia", "Ib"):
+                lo = HALF * (tok == "Ib")
+                interleave(last, lo, lo + HALF, True)
+            elif tok in ("Qa", "Qb"):
+                lo = HALF * (tok == "Qb")
+                quantize(last, lo, lo + HALF)
             elif tok.startswith("I") and len(tok) == 4:
                 interleave(unit(tok[1:4]), 0, CHUNK, True)
             elif tok.startswith("I") and tok[4] == "v":
@@ -366,14 +342,8 @@ def tile_multiscaleretention_pa_kernel(tc, x, sin, cos, Wq_bytes, Wq_scale, Wk, 
                 return ["I" + tok[1]]
             if tok.startswith("Mpre"):
                 return ["xQ", "Q%s%d%s" % (last_ch[0], last_ch[1], tok[4])]
-            if tok.startswith("M2_"):
-                return ["E1_" + tok[3], "R"]
             if tok.startswith("P"):
                 return ["Mpre1", "Q" + tok[1]]
-            if tok.startswith("E1_"):
-                return ["P" + tok[3]]
-            if tok.startswith("E2_"):
-                return ["M2_" + tok[3]]
             if tok.startswith("M1"):
                 older = chunks.index((tok[2], int(tok[3]))) - 2
                 return ["xQ"] + ["Q%s%d" % (tok[2:4], g) for g in range(PASSES)] + (["E1%s%d" % chunks[older]] if older >= 0 else [])
@@ -382,8 +352,8 @@ def tile_multiscaleretention_pa_kernel(tc, x, sin, cos, Wq_bytes, Wq_scale, Wk, 
                 return ["E1" + tok[2:4], "R"] + (["E2%s%d" % chunks[older]] if older >= 0 else [])
             if tok.startswith("E"):
                 return ["M" + tok[1:4]]
-            if tok == "F":
-                return ["C"] + ["P%d" % j for j in X_STATIONARY]
+            if tok.startswith("F"):
+                return ["C", "P" + tok[1]]
             return []
 
         with tc.manual_schedule():

@@ -30,8 +30,8 @@ FLOPS = 2 * 2 * B * E * HK
 
 VECTOR = (
     "Wq00.0 Wq00.1 Wq00.2 Iq00 Ik00 Qq00 Iq01 Qk00 Iq02 Qq01 Ik01 xQ Qq02 R Ik02 Qk01 Iq10 Qk02 Iq11 Qq10 "
-    "Ik10v0 Qq11 Iq12 Qk10 Ik11 Qq12 Iq20 Qk11 Ik12 Qq20 Iq21 Qk12 Iq22v0 Qq21 Ia Qq22 Ik21v0 Ib Qk20 Qa "
-    "Qk21 Qb Fa Fb"
+    "Ik10v0 Qq11 Iq12 Qk10 Ik11 Qq12 Iq20 Qk11 Ik12 Qq20 Iq21 Qk12 Iq22v0 Qq21 Ia Qq22 Ik21v0 Ib Qk20 "
+    "Qk21 Qa Qb Fa Fb"
 )
 SCALAR = (
     "Wq00.3 Wq01.0 Wq01.1 Wq01.2 Wq01.3 Wq02.0 Wq02.1 Wq02.2 Wq02.3 xE0 xE1 xE2 C Wq10.0 Wq10.1 Wq10.2 "
@@ -42,7 +42,7 @@ SCALAR = (
 TENSOR = (
     "B xT M1q0 M2q0 M1k0 M2k0 M1q1 M2q1 M1k1 M1q2 M2k1 Mpre0 Mpre1 Pa Pb M2q2"
 )
-LOADS = "c s q00 q01 k00 q02 x k01 q10 k02 q11 k10 q12 k11 q20 k12 q21 q22 k20 k21 k22"
+LOADS = "s q00 q01 c k00 q02 x k01 q10 k02 q11 k10 q12 k11 q20 k12 q21 q22 k20 k21 k22"
 
 
 def tile_multiscaleretention_pa_kernel(tc, x, sin, cos, Wq_bytes, Wq_scale, Wk, out_0, out_1):

@@ -34,13 +34,13 @@ VECTOR = (
     "Qk21 Qa Qb Fa Fb"
 )
 SCALAR = (
-    "Wq00.3 Wq01.0 Wq01.1 Wq01.2 Wq01.3 Wq02.0 Wq02.1 Wq02.2 Wq02.3 xE0 xE1 xE2 C Wq10.0 Wq10.1 Wq10.2 "
+    "Wq00.3 Wq01.0 Wq01.1 Wq01.2 Wq01.3 Wq02.0 Wq02.1 Wq02.2 Wq02.3 xE0 xE1 xE2 Wq10.0 C Wq10.1 Wq10.2 "
     "Wq10.3 Wq11.0 Wq11.1 Wq11.2 Wq11.3 Ik10.1 E1q0 Wq12.0 Wq12.1 Wq12.2 Wq12.3 Wq20.0 Wq20.1 E1k0 E2q0 "
     "Wq20.2 Wq20.3 Wq21.0 E2k0 Wq21.1 Wq21.2 Wq21.3 Wq22.0 Wq22.1 Wq22.2 E1q1 Wq22.3 Iq22.1 Ik20.0 E2q1 "
     "Ik20.1 E1k1 Ik21.1 E1q2 E2k1 E2q2"
 )
 TENSOR = (
-    "B xT M1q0 M2q0 M1k0 M2k0 M1q1 M2q1 M1k1 M1q2 M2k1 Mpre0 Mpre1 Pa Pb M2q2"
+    "xT B M1q0 M2q0 M1k0 M2k0 M1q1 M2q1 M1k1 M1q2 M2k1 Mpre0 Mpre1 Pa Pb M2q2"
 )
 LOADS = "s q00 q01 c k00 q02 x k01 q10 k02 q11 k10 q12 k11 q20 k12 q21 q22 k20 k21 k22"
 
@@ -104,11 +104,8 @@ def tile_multiscaleretention_pa_kernel(tc, x, sin, cos, Wq_bytes, Wq_scale, Wk, 
         ident = idsw[:, 0, :]
         id_pairs = idsw[:, 0, :].rearrange("p (i two) -> p i two", two=2)
         sw_pairs = idsw[:, 1, :].rearrange("p (i two) -> p i two", two=2)
-        nc.gpsimd.tensor_copy(out=sw_pairs[:, :, 0], in_=id_pairs[:, :, 1])
+        nc.gpsimd.tensor_scalar(out=sw_pairs[:, :, 0], in0=id_pairs[:, :, 1], scalar1=-1.0, scalar2=None, op0=ALU.mult)
         nc.gpsimd.tensor_copy(out=sw_pairs[:, :, 1], in_=id_pairs[:, :, 0])
-        nc.gpsimd.tensor_scalar(
-            out=cs_row[:, DK : 2 * DK : 2], in0=cs_row[:, DK : 2 * DK : 2], scalar1=-1.0, scalar2=None, op0=ALU.mult
-        )
 
         warm = keep.tile([P, 2], F32, name="warm")
         nc.vector.memset(warm[:, 0:1], 0.0)
@@ -233,6 +230,7 @@ def tile_multiscaleretention_pa_kernel(tc, x, sin, cos, Wq_bytes, Wq_scale, Wk, 
 
         def build_cs():
             nc.scalar.copy(out=cs[:].rearrange("p s d -> p (s d)"), in_=spread["cs"][:])
+            nc.scalar.activation(out=cs[:, 1, 0:DK:2], in_=spread["cs"][:, DK : 2 * DK : 2], func=ACT.Copy, scale=-1.0)
 
         def rotate_last(half):
             m, c = last_ch

@@ -25,22 +25,23 @@ CHUNKS = HK // CHUNK
 TILES = CHUNK // P
 
 HALF = CHUNK // 2
+PARTS = ((0, HALF), (HALF, CHUNK))
 
 FLOPS = 2 * 2 * B * E * HK
 
 VECTOR = (
-    "Wq00.0 Wq00.1 Wq00.2 Iq00 Ik00 Qq00 Iq01 Qk00 Iq02 Qq01 Ik01 xQ Qq02 R Ik02 Qk01 Iq10 Qk02 Iq11 Qq10 "
-    "Ik10v0 Qq11 Iq12 Qk10 Ik11 Qq12 Iq20 Qk11 Ik12 Qq20 Iq21 Qk12 Iq22v0 Qq21 Ia Qq22 Ik21v0 Ib Qk20 "
-    "Qk21 Qa Qb Fa Fb"
+    "Z Wq00.0 Wq00.1 Wq00.2 Iq00 Ik00 Qq00 Iq01 Qk00 Iq02 Qq01 Ik01 xQ Qq02 R Ik02 Qk01 Iq10 Qk02 Iq11 "
+    "Qq10 Ik10v0 Qq11 Iq12 Qk10 Ik11 Qq12 Iq20 Qk11 Ik12 Qq20 Iq21 Qk12 Iq22v0 Qq21 Ia Qq22 Ik21v0 Ib "
+    "Qk20 Qk21 Qa Qb F0 G0 F1 G1"
 )
 SCALAR = (
     "Wq00.3 Wq01.0 Wq01.1 Wq01.2 Wq01.3 Wq02.0 Wq02.1 Wq02.2 Wq02.3 xE0 xE1 xE2 Wq10.0 C Wq10.1 Wq10.2 "
     "Wq10.3 Wq11.0 Wq11.1 Wq11.2 Wq11.3 Ik10.1 E1q0 Wq12.0 Wq12.1 Wq12.2 Wq12.3 Wq20.0 Wq20.1 E1k0 E2q0 "
     "Wq20.2 Wq20.3 Wq21.0 E2k0 Wq21.1 Wq21.2 Wq21.3 Wq22.0 Wq22.1 Wq22.2 E1q1 Wq22.3 Iq22.1 Ik20.0 E2q1 "
-    "Ik20.1 E1k1 Ik21.1 E1q2 E2k1 E2q2"
+    "Ik20.1 E1k1 Ik21.1 E1q2 E2k1 E2q2a E2q2b"
 )
 TENSOR = (
-    "xT B M1q0 M2q0 M1k0 M2k0 M1q1 M2q1 M1k1 M1q2 M2k1 Mpre0 Mpre1 Pa Pb M2q2"
+    "xT B M1q0 M2q0 M1k0 M2k0 M1q1 M2q1 M1k1 M1q2 M2k1 Mpre0 Mpre1 Pa Pb M2q2a M2q2b"
 )
 LOADS = "s q00 q01 c k00 q02 x k01 q10 k02 q11 k10 q12 k11 q20 k12 q21 q22 k20 k21 k22"
 
@@ -104,8 +105,6 @@ def tile_multiscaleretention_pa_kernel(tc, x, sin, cos, Wq_bytes, Wq_scale, Wk, 
         ident = idsw[:, 0, :]
         id_pairs = idsw[:, 0, :].rearrange("p (i two) -> p i two", two=2)
         sw_pairs = idsw[:, 1, :].rearrange("p (i two) -> p i two", two=2)
-        nc.gpsimd.tensor_scalar(out=sw_pairs[:, :, 0], in0=id_pairs[:, :, 1], scalar1=-1.0, scalar2=None, op0=ALU.mult)
-        nc.gpsimd.tensor_copy(out=sw_pairs[:, :, 1], in_=id_pairs[:, :, 0])
 
         warm = keep.tile([P, 2], F32, name="warm")
         nc.vector.memset(warm[:, 0:1], 0.0)
@@ -193,17 +192,17 @@ def tile_multiscaleretention_pa_kernel(tc, x, sin, cos, Wq_bytes, Wq_scale, Wk, 
                         stop=(g == PASSES - 1),
                     )
 
-        def x_stationary(half, g):
-            if half not in acc:
-                acc_t = pst.tile([P, HALF], F32, name="acc_t", tag="bank")
-                acc[half] = acc_t
-            cols = slice(half * HALF, (half + 1) * HALF)
+        def last_passes(part, g):
+            lo, hi = PARTS[part]
+            if part not in acc:
+                acc_t = pst.tile([P, hi - lo], F32, name="acc_t", tag="bank")
+                acc[part] = acc_t
             nc.tensor.matmul_mx(
-                out=acc[half][:],
+                out=acc[part][:],
                 lhsT=x_codes[:, g, :].bitcast(FP8X4),
                 lhsT_scale=x_scales[:, g, :],
-                rhs=codes[last_ch][:, g, cols].bitcast(FP8X4),
-                rhs_scale=scales[last_ch][:, g, cols],
+                rhs=codes[last_ch][:, g, lo:hi].bitcast(FP8X4),
+                rhs_scale=scales[last_ch][:, g, lo:hi],
                 start=(g == 0),
                 stop=(g == PASSES - 1),
             )
@@ -213,18 +212,18 @@ def tile_multiscaleretention_pa_kernel(tc, x, sin, cos, Wq_bytes, Wq_scale, Wk, 
             nc.scalar.copy(out=qt[:], in_=acc[ch][:])
             qts[ch] = qt
 
-        def rotate(ch):
+        def rotate(ch, tiles):
             tu = ps2.tile([P, CHUNK], F32, name="turned")
-            for j in range(TILES):
+            turned[(ch, tiles[0] * P)] = tu
+            for j in tiles:
                 cols = slice(j * P, (j + 1) * P)
                 nc.tensor.matmul(out=tu[:, cols], lhsT=qts[ch][:, cols], rhs=rot[:], start=True, stop=True)
-            turned[ch] = tu
 
-        def store(ch):
+        def store(ch, lo, hi):
             m, c = ch
             res = res_pool.tile([P, CHUNK], F32, name="res")
-            nc.scalar.copy(out=res[:], in_=turned[ch][:])
-            nc.sync.dma_start(out=outs[m][:, c * CHUNK : (c + 1) * CHUNK], in_=res[:])
+            nc.scalar.copy(out=res[:, lo:hi], in_=turned[(ch, lo)][:, lo:hi])
+            nc.sync.dma_start(out=outs[m][:, c * CHUNK + lo : c * CHUNK + hi], in_=res[:, lo:hi])
 
         cs = keep.tile([P, 2, DK], F32, name="cs")
 
@@ -232,29 +231,34 @@ def tile_multiscaleretention_pa_kernel(tc, x, sin, cos, Wq_bytes, Wq_scale, Wk, 
             nc.scalar.copy(out=cs[:].rearrange("p s d -> p (s d)"), in_=spread["cs"][:])
             nc.scalar.activation(out=cs[:, 1, 0:DK:2], in_=spread["cs"][:, DK : 2 * DK : 2], func=ACT.Copy, scale=-1.0)
 
-        def rotate_last(half):
-            m, c = last_ch
-            heads = HALF // DK
-            straight = keep.tile([P, HALF], F32, name="straight%d" % half)
-            crossed = keep.tile([P, HALF], F32, name="crossed%d" % half)
-            res = res_pool.tile([P, CHUNK], F32, name="res")
+        def products(part):
+            width = acc[part].shape[1]
+            heads = width // DK
+            straight = keep.tile([P, width], F32, name="straight%d" % part)
+            crossed = keep.tile([P, width], F32, name="crossed%d" % part)
             nc.vector.tensor_tensor(
                 out=straight[:].rearrange("p (h d) -> p h d", h=heads),
-                in0=acc[half][:].rearrange("p (h d) -> p h d", h=heads),
+                in0=acc[part][:].rearrange("p (h d) -> p h d", h=heads),
                 in1=cs[:, 0, :].unsqueeze(1).to_broadcast([P, heads, DK]),
                 op=ALU.mult,
             )
             nc.vector.tensor_tensor(
                 out=crossed[:].rearrange("p (h i two) -> p h i two", h=heads, two=2),
-                in0=acc[half][:].rearrange("p (h i two) -> p h i two", h=heads, two=2)[:, :, :, ::-1],
+                in0=acc[part][:].rearrange("p (h i two) -> p h i two", h=heads, two=2)[:, :, :, ::-1],
                 in1=cs[:, 1, :].rearrange("p (i two) -> p i two", two=2).unsqueeze(1).to_broadcast([P, heads, DK // 2, 2]),
                 op=ALU.mult,
             )
-            adder = nc.gpsimd if half == 0 else nc.vector
-            adder.tensor_tensor(out=res[:, :HALF], in0=straight[:], in1=crossed[:], op=ALU.add)
-            lo = c * CHUNK + half * HALF
-            nc.sync.dma_start(out=outs[m][:, lo : lo + HALF], in_=res[:, :HALF])
+            terms[part] = (straight, crossed)
 
+        def finish(part):
+            m, c = last_ch
+            lo, hi = PARTS[part]
+            res = res_pool.tile([P, CHUNK], F32, name="res")
+            adder = nc.gpsimd if part == 0 else nc.vector
+            adder.tensor_tensor(out=res[:, lo:hi], in0=terms[part][0][:], in1=terms[part][1][:], op=ALU.add)
+            nc.sync.dma_start(out=outs[m][:, c * CHUNK + lo : c * CHUNK + hi], in_=res[:, lo:hi])
+
+        terms = {}
         last = ("k", CHUNKS - 1, PASSES - 1)
         last_ch = (last[0], last[1])
         xts = {}
@@ -280,25 +284,31 @@ def tile_multiscaleretention_pa_kernel(tc, x, sin, cos, Wq_bytes, Wq_scale, Wk, 
                 cs_all = pst.tile([P, 2 * DK], F32, name="cs_all", tag="bank")
                 nc.tensor.matmul(out=cs_all[:], lhsT=ones[:], rhs=cs_row[:], start=True, stop=True)
                 spread["cs"] = cs_all
+            elif tok == "Z":
+                nc.vector.tensor_scalar(out=sw_pairs[:, :, 0], in0=id_pairs[:, :, 1], scalar1=-1.0, scalar2=None, op0=ALU.mult)
+                nc.vector.tensor_copy(out=sw_pairs[:, :, 1], in_=id_pairs[:, :, 0])
             elif tok == "R":
                 build_rot()
             elif tok == "C":
                 build_cs()
-            elif tok in ("Fa", "Fb"):
-                rotate_last("ab".index(tok[1]))
+            elif tok.startswith("F"):
+                products(int(tok[1]))
+            elif tok.startswith("G"):
+                finish(int(tok[1]))
             elif tok.startswith("Mpre"):
-                for half in range(2):
-                    x_stationary(half, int(tok[4]))
+                for part in range(len(PARTS)):
+                    last_passes(part, int(tok[4]))
             elif tok in ("Pa", "Pb"):
-                x_stationary("ab".index(tok[1]), PASSES - 1)
+                last_passes("ab".index(tok[1]), PASSES - 1)
             elif tok.startswith("M1"):
                 passes((tok[2], int(tok[3])))
             elif tok.startswith("E1"):
                 copy_out((tok[2], int(tok[3])))
             elif tok.startswith("M2"):
-                rotate((tok[2], int(tok[3])))
+                rotate((tok[2], int(tok[3])), {"": (0, 1, 2, 3), "a": (0, 1), "b": (2, 3)}[tok[4:]])
             elif tok.startswith("E2"):
-                store((tok[2], int(tok[3])))
+                lo, hi = {"": (0, CHUNK), "a": (0, HALF), "b": (HALF, CHUNK)}[tok[4:]]
+                store((tok[2], int(tok[3])), lo, hi)
             elif tok.startswith("W"):
                 widen(unit(tok[1:4]), int(tok[5]), tok in VECTOR.split())
             elif tok in ("Ia", "Ib"):
@@ -330,7 +340,9 @@ def tile_multiscaleretention_pa_kernel(tc, x, sin, cos, Wq_bytes, Wq_scale, Wk, 
                 return ["xT"]
             if tok == "xQ":
                 return ["xE%d" % g for g in range(PASSES)]
-            if tok in ("R", "C"):
+            if tok == "R":
+                return ["B", "Z"]
+            if tok == "C":
                 return ["B"]
             if tok.startswith("Iq"):
                 return [n for n in names if n.startswith("W" + u)]
@@ -347,11 +359,13 @@ def tile_multiscaleretention_pa_kernel(tc, x, sin, cos, Wq_bytes, Wq_scale, Wk, 
                 return ["xQ"] + ["Q%s%d" % (tok[2:4], g) for g in range(PASSES)] + (["E1%s%d" % chunks[older]] if older >= 0 else [])
             if tok.startswith("M2"):
                 older = chunks.index((tok[2], int(tok[3]))) - 2
-                return ["E1" + tok[2:4], "R"] + (["E2%s%d" % chunks[older]] if older >= 0 else [])
+                return ["E1" + tok[2:4], "R"] + (["E2%s%d" % chunks[older]] if older >= 0 else []) + (["E2k1"] if tok == "M2q2b" else [])
             if tok.startswith("E"):
-                return ["M" + tok[1:4]]
+                return ["M" + tok[1:]]
             if tok.startswith("F"):
-                return ["C", "P" + tok[1]]
+                return ["C", "P" + "ab"[int(tok[1])]]
+            if tok.startswith("G"):
+                return ["F" + tok[1]]
             return []
 
         with tc.manual_schedule():

@@ -30,20 +30,20 @@ PARTS = ((0, HALF), (HALF, CHUNK))
 FLOPS = 2 * 2 * B * E * HK
 
 VECTOR = (
-    "Z Wq00.0 Wq00.1 Wq00.2 Iq00 Ik00 Qq00 Iq01 Qk00 Iq02 Qq01 Ik01 xQ Qq02 R Ik02 Qk01 Iq10 Qk02 Iq11 "
-    "Qq10 Ik10v0 Qq11 Iq12 Qk10 Ik11 Qq12 Iq20 Qk11 Ik12 Qq20 Iq21 Qk12 Iq22v0 Qq21 Ia Qq22 Ik21v0 Ib "
-    "Qk20 Qk21 Qa Qb F0 G0 F1 G1"
+    "Z Wq00.0 Wq00.1 Wq00.2 Wq01.0 Iq00 Ik00 Qq00 Iq01 Qk00 Iq02 Qq01 Ik01 xQ R0 Qq02 R1 Ik02 Qk01 Iq10 "
+    "Qk02 Iq11 Qq10 Ik10v0 Qq11 Iq12 Qk10 Ik11 Qq12 Iq20 Qk11 Ik12 Qq20 Iq21 Qk12 Iq22v0 Qq21 Ia Qq22 "
+    "Ik21v0 Ib Qk20 Qk21 Qa Qb F0 F1 G0 G1"
 )
 SCALAR = (
-    "Wq00.3 Wq01.0 Wq01.1 Wq01.2 Wq01.3 Wq02.0 Wq02.1 Wq02.2 Wq02.3 xE0 xE1 xE2 Wq10.0 C Wq10.1 Wq10.2 "
-    "Wq10.3 Wq11.0 Wq11.1 Wq11.2 Wq11.3 Ik10.1 E1q0 Wq12.0 Wq12.1 Wq12.2 Wq12.3 Wq20.0 Wq20.1 E1k0 E2q0 "
-    "Wq20.2 Wq20.3 Wq21.0 E2k0 Wq21.1 Wq21.2 Wq21.3 Wq22.0 Wq22.1 Wq22.2 E1q1 Wq22.3 Iq22.1 Ik20.0 E2q1 "
-    "Ik20.1 E1k1 Ik21.1 E1q2 E2k1 E2q2a E2q2b"
+    "Wq00.3 Wq01.1 Wq01.2 Wq01.3 Wq02.0 Wq02.1 Wq02.2 Wq02.3 xE0 xE1 xE2 Wq10.0 C Wq10.1 Wq10.2 Wq10.3 "
+    "Wq11.0 Wq11.1 Wq11.2 Wq11.3 Ik10.1 Wq12.0 E1q0 Wq12.1 Wq12.2 Wq12.3 Wq20.0 Wq20.1 E1k0 E2q0 Wq20.2 "
+    "Wq20.3 Wq21.0 E2k0 Wq21.1 Wq21.2 Wq21.3 Wq22.0 Wq22.1 Wq22.2 E1q1 Wq22.3 Iq22.1 Ik20.0 Ik20.1 E1k1 "
+    "Ik21.1 E1q2 E2q1 E2k1 E2q2a E2q2b"
 )
 TENSOR = (
     "xT B M1q0 M2q0 M1k0 M2k0 M1q1 M2q1 M1k1 M1q2 M2k1 Mpre0 Mpre1 Pa Pb M2q2a M2q2b"
 )
-LOADS = "s q00 q01 c k00 q02 x k01 q10 k02 q11 k10 q12 k11 q20 k12 q21 q22 k20 k21 k22"
+LOADS = "s q00 q01 k00 q02 c x k01 q10 k02 q11 k10 q12 k11 q20 k12 q21 q22 k20 k21 k22"
 
 
 def tile_multiscaleretention_pa_kernel(tc, x, sin, cos, Wq_bytes, Wq_scale, Wk, out_0, out_1):
@@ -117,15 +117,7 @@ def tile_multiscaleretention_pa_kernel(tc, x, sin, cos, Wq_bytes, Wq_scale, Wk, 
 
         spread = {}
 
-        def build_rot():
-            prod = keep.tile([P, 2, P], F32, name="prod")
-            nc.vector.tensor_tensor(
-                out=prod[:].rearrange("p s (h d) -> p s h d", h=2),
-                in0=idsw[:].rearrange("p s (h d) -> p s h d", h=2),
-                in1=spread["cs"][:].rearrange("p (s d) -> p s d", s=2).unsqueeze(2).to_broadcast([P, 2, 2, DK]),
-                op=ALU.mult,
-            )
-            nc.vector.tensor_tensor(out=rot[:], in0=prod[:, 0, :], in1=prod[:, 1, :], op=ALU.add)
+        prod = keep.tile([P, 2, P], F32, name="prod")
 
         codes = {}
         scales = {}
@@ -254,8 +246,7 @@ def tile_multiscaleretention_pa_kernel(tc, x, sin, cos, Wq_bytes, Wq_scale, Wk, 
             m, c = last_ch
             lo, hi = PARTS[part]
             res = res_pool.tile([P, CHUNK], F32, name="res")
-            adder = nc.gpsimd if part == 0 else nc.vector
-            adder.tensor_tensor(out=res[:, lo:hi], in0=terms[part][0][:], in1=terms[part][1][:], op=ALU.add)
+            nc.vector.tensor_tensor(out=res[:, lo:hi], in0=terms[part][0][:], in1=terms[part][1][:], op=ALU.add)
             nc.sync.dma_start(out=outs[m][:, c * CHUNK + lo : c * CHUNK + hi], in_=res[:, lo:hi])
 
         terms = {}
@@ -287,8 +278,15 @@ def tile_multiscaleretention_pa_kernel(tc, x, sin, cos, Wq_bytes, Wq_scale, Wk, 
             elif tok == "Z":
                 nc.vector.tensor_scalar(out=sw_pairs[:, :, 0], in0=id_pairs[:, :, 1], scalar1=-1.0, scalar2=None, op0=ALU.mult)
                 nc.vector.tensor_copy(out=sw_pairs[:, :, 1], in_=id_pairs[:, :, 0])
-            elif tok == "R":
-                build_rot()
+            elif tok == "R0":
+                nc.vector.tensor_tensor(
+                    out=prod[:].rearrange("p s (h d) -> p s h d", h=2),
+                    in0=idsw[:].rearrange("p s (h d) -> p s h d", h=2),
+                    in1=spread["cs"][:].rearrange("p (s d) -> p s d", s=2).unsqueeze(2).to_broadcast([P, 2, 2, DK]),
+                    op=ALU.mult,
+                )
+            elif tok == "R1":
+                nc.vector.tensor_tensor(out=rot[:], in0=prod[:, 0, :], in1=prod[:, 1, :], op=ALU.add)
             elif tok == "C":
                 build_cs()
             elif tok.startswith("F"):
@@ -340,8 +338,10 @@ def tile_multiscaleretention_pa_kernel(tc, x, sin, cos, Wq_bytes, Wq_scale, Wk, 
                 return ["xT"]
             if tok == "xQ":
                 return ["xE%d" % g for g in range(PASSES)]
-            if tok == "R":
+            if tok == "R0":
                 return ["B", "Z"]
+            if tok == "R1":
+                return ["R0"]
             if tok == "C":
                 return ["B"]
             if tok.startswith("Iq"):
@@ -359,7 +359,7 @@ def tile_multiscaleretention_pa_kernel(tc, x, sin, cos, Wq_bytes, Wq_scale, Wk, 
                 return ["xQ"] + ["Q%s%d" % (tok[2:4], g) for g in range(PASSES)] + (["E1%s%d" % chunks[older]] if older >= 0 else [])
             if tok.startswith("M2"):
                 older = chunks.index((tok[2], int(tok[3]))) - 2
-                return ["E1" + tok[2:4], "R"] + (["E2%s%d" % chunks[older]] if older >= 0 else []) + (["E2k1"] if tok == "M2q2b" else [])
+                return ["E1" + tok[2:4], "R1"] + (["E2%s%d" % chunks[older]] if older >= 0 else []) + (["E2k1"] if tok == "M2q2b" else [])
             if tok.startswith("E"):
                 return ["M" + tok[1:]]
             if tok.startswith("F"):

@@ -31,14 +31,14 @@ FLOPS = 2 * 2 * B * E * HK
 
 VECTOR = (
     "Z Wq00.0 Wq00.1 Wq00.2 Wq01.0 Iq00 Ik00 Qq00 Iq01 Qk00 Iq02 Qq01 Ik01 xQ R0 Qq02 R1 Ik02 Qk01 Iq10 "
-    "Qk02 Iq11 Qq10 Ik10v0 Qq11 Iq12 Qk10 Ik11 Qq12 Iq20 Qk11 Ik12 Qq20 Iq21 Qk12 Iq22v0 Qq21 Ia Qq22 "
+    "Qk02 Iq11 Qq10 Ik10v0 Qq11 Iq12 Qk10 Ik11v0 Qq12 Iq20 Qk11 Ik12 Qq20 Iq21 Qk12 Iq22v0 Qq21 Ia Qq22 "
     "Ik21v0 Ib Qk20 Qk21 Qa Qb F0 F1 G0 G1"
 )
 SCALAR = (
     "Wq00.3 Wq01.1 Wq01.2 Wq01.3 Wq02.0 Wq02.1 Wq02.2 Wq02.3 xE0 xE1 xE2 Wq10.0 C Wq10.1 Wq10.2 Wq10.3 "
-    "Wq11.0 Wq11.1 Wq11.2 Wq11.3 Ik10.1 Wq12.0 E1q0 Wq12.1 Wq12.2 Wq12.3 Wq20.0 Wq20.1 E1k0 E2q0 Wq20.2 "
-    "Wq20.3 Wq21.0 E2k0 Wq21.1 Wq21.2 Wq21.3 Wq22.0 Wq22.1 Wq22.2 E1q1 Wq22.3 Iq22.1 Ik20.0 Ik20.1 E1k1 "
-    "Ik21.1 E1q2 E2q1 E2k1 E2q2a E2q2b"
+    "Wq11.0 Wq11.1 Wq11.2 Wq11.3 Ik10.1 Wq12.0 E1q0 Wq12.1 Wq12.2 Wq12.3 Ik11.1 Wq20.0 Wq20.1 E1k0 E2q0 "
+    "Wq20.2 Wq20.3 Wq21.0 Wq21.1 Wq21.2 Wq21.3 Wq22.0 Wq22.1 Wq22.2 E1q1 Wq22.3 Iq22.1 Ik20.0 Ik20.1 E1k1 "
+    "Ik21.1 E1q2 E2k0 E2q1 E2k1 E2q2a E2q2b"
 )
 TENSOR = (
     "xT B M1q0 M2q0 M1k0 M2k0 M1q1 M2q1 M1k1 M1q2 M2k1 Mpre0 Mpre1 Pa Pb M2q2a M2q2b"
@@ -64,9 +64,9 @@ def tile_multiscaleretention_pa_kernel(tc, x, sin, cos, Wq_bytes, Wq_scale, Wk, 
         grp_pool = ctx.enter_context(tc.tile_pool(name="grp", bufs=10))
         qt_pool = ctx.enter_context(tc.tile_pool(name="qt", bufs=3))
         res_pool = ctx.enter_context(tc.tile_pool(name="res", bufs=9))
-        pst = ctx.enter_context(tc.psum_pool(name="pst", bufs=4))
+        pst = ctx.enter_context(tc.psum_pool(name="pst", bufs=3))
         ps1 = ctx.enter_context(tc.psum_pool(name="ps1", bufs=2))
-        ps2 = ctx.enter_context(tc.psum_pool(name="ps2", bufs=2))
+        ps2 = ctx.enter_context(tc.psum_pool(name="ps2", bufs=3))
 
         raw = {}
 
@@ -332,6 +332,8 @@ def tile_multiscaleretention_pa_kernel(tc, x, sin, cos, Wq_bytes, Wq_scale, Wk, 
         names = [q for queue in queues for q in queue]
         written = set()
 
+        turns = [n[2:] for n in TENSOR.split() if n.startswith("M2")]
+
         def needs(tok):
             u = tok[1:4]
             if tok.startswith("xE"):
@@ -358,8 +360,10 @@ def tile_multiscaleretention_pa_kernel(tc, x, sin, cos, Wq_bytes, Wq_scale, Wk, 
                 older = chunks.index((tok[2], int(tok[3]))) - 2
                 return ["xQ"] + ["Q%s%d" % (tok[2:4], g) for g in range(PASSES)] + (["E1%s%d" % chunks[older]] if older >= 0 else [])
             if tok.startswith("M2"):
-                older = chunks.index((tok[2], int(tok[3]))) - 2
-                return ["E1" + tok[2:4], "R1"] + (["E2%s%d" % chunks[older]] if older >= 0 else []) + (["E2k1"] if tok == "M2q2b" else [])
+                older = turns.index(tok[2:]) - 3
+                return ["E1" + tok[2:4], "R1"] + (["E2" + turns[older]] if older >= 0 else [])
+            if tok == "B":
+                return ["xE0"]
             if tok.startswith("E"):
                 return ["M" + tok[1:]]
             if tok.startswith("F"):

@@ -31,14 +31,14 @@ FLOPS = 2 * 2 * B * E * HK
 
 VECTOR = (
     "Z Wq00.0 Wq00.1 Wq00.2 Wq01.0 Iq00 Ik00 Qq00 Iq01 Qk00 Iq02 Qq01 Ik01 xQ R0 Qq02 R1 Ik02 Qk01 Iq10 "
-    "Qk02 Iq11 Qq10 Ik10v0 Qq11 Iq12 Qk10 Ik11v0 Qq12 Iq20 Qk11 Ik12 Qq20 Iq21 Qk12 Iq22v0 Qq21 Ia Qq22 "
+    "Qk02 Iq11 Qq10 Ik10v0 Qq11 Iq12 Qk10 Ik11 Qq12 Iq20 Qk11 Ik12w Qq20 Iq21 Qk12 Iq22v0 Qq21 Ia Qq22 "
     "Ik21v0 Ib Qk20 Qk21 Qa Qb F0 F1 G0 G1"
 )
 SCALAR = (
-    "Wq00.3 Wq01.1 Wq01.2 Wq01.3 Wq02.0 Wq02.1 Wq02.2 Wq02.3 xE0 xE1 xE2 Wq10.0 C Wq10.1 Wq10.2 Wq10.3 "
-    "Wq11.0 Wq11.1 Wq11.2 Wq11.3 Ik10.1 Wq12.0 E1q0 Wq12.1 Wq12.2 Wq12.3 Ik11.1 Wq20.0 Wq20.1 E1k0 E2q0 "
-    "Wq20.2 Wq20.3 Wq21.0 Wq21.1 Wq21.2 Wq21.3 Wq22.0 Wq22.1 Wq22.2 E1q1 Wq22.3 Iq22.1 Ik20.0 Ik20.1 E1k1 "
-    "Ik21.1 E1q2 E2k0 E2q1 E2k1 E2q2a E2q2b"
+    "Wq00.3 Wq01.1 Wq01.2 Wq01.3 Wq02.0 Wq02.1 Wq02.2 Wq02.3 xE0 xE1 xE2 Wq10.0 Wq10.1 Wq10.2 Wq10.3 "
+    "Wq11.0 Wq11.1 Wq11.2 Wq11.3 Ik10.1 Wq12.0 Wq12.1 E1q0 Wq12.2 Wq12.3 Wq20.0 Wq20.1 Wq20.2 E1k0 E2q0 "
+    "Wq20.3 Wq21.0 Wq21.1 Wq21.2 Wq21.3 Ik12z Wq22.0 Wq22.1 Wq22.2 Wq22.3 E1q1 Iq22.1 Ik20.0 Ik20.1 E1k1 "
+    "Ik21.1 E1q2 C E2k0 E2q1 E2k1 E2q2a E2q2b"
 )
 TENSOR = (
     "xT B M1q0 M2q0 M1k0 M2k0 M1q1 M2q1 M1k1 M1q2 M2k1 Mpre0 Mpre1 Pa Pb M2q2a M2q2b"
@@ -317,6 +317,10 @@ def tile_multiscaleretention_pa_kernel(tc, x, sin, cos, Wq_bytes, Wq_scale, Wk, 
                 quantize(last, lo, lo + HALF)
             elif tok.startswith("I") and len(tok) == 4:
                 interleave(unit(tok[1:4]), 0, CHUNK, True)
+            elif tok.startswith("I") and tok[4] in "wz":
+                cut = 3 * CHUNK // 4
+                lo, hi = (0, cut) if tok[4] == "w" else (cut, CHUNK)
+                interleave(unit(tok[1:4]), lo, hi, tok[4] == "w")
             elif tok.startswith("I") and tok[4] == "v":
                 h = int(tok[5])
                 interleave(unit(tok[1:4]), h * CHUNK // 2, (h + 1) * CHUNK // 2, True)

@@ -35,15 +35,15 @@ VECTOR = (
     "Ik21v0 Ib Qk20 Qk21 Qa Qb F0 F1 G0 G1"
 )
 SCALAR = (
-    "Wq00.3 Wq01.1 Wq01.2 Wq01.3 Wq02.0 Wq02.1 Wq02.2 Wq02.3 xE0 xE1 xE2 Wq10.0 Wq10.1 Wq10.2 Wq10.3 "
-    "Wq11.0 Wq11.1 Wq11.2 Wq11.3 Ik10.1 Wq12.0 Wq12.1 E1q0 Wq12.2 Wq12.3 Wq20.0 Wq20.1 Wq20.2 E1k0 E2q0 "
+    "Wq00.3 Wq01.1 Wq01.2 Wq01.3 Wq02.0 Wq02.1 Wq02.2 Wq02.3 Wq10.0 Wq10.1 Wq10.2 Wq10.3 xE0 xE1 xE2 "
+    "Wq11.0 Wq11.1 Wq11.2 Wq11.3 Wq12.0 Wq12.1 Wq12.2 Wq12.3 E1q0 Ik10.1 Wq20.0 Wq20.1 Wq20.2 E1k0 E2q0 "
     "Wq20.3 Wq21.0 Wq21.1 Wq21.2 Wq21.3 Ik12z Wq22.0 Wq22.1 Wq22.2 Wq22.3 E1q1 Iq22.1 Ik20.0 Ik20.1 E1k1 "
     "Ik21.1 E1q2 C E2k0 E2q1 E2k1 E2q2a E2q2b"
 )
 TENSOR = (
     "xT B M1q0 M2q0 M1k0 M2k0 M1q1 M2q1 M1k1 M1q2 M2k1 Mpre0 Mpre1 Pa Pb M2q2a M2q2b"
 )
-LOADS = "s q00 q01 k00 q02 c x k01 q10 k02 q11 k10 q12 k11 q20 k12 q21 q22 k20 k21 k22"
+LOADS = "s q00 q01 k00 q02 q10 x c k01 q11 k02 q12 k10 q20 k11 k12 q21 q22 k20 k21 k22"
 
 
 def tile_multiscaleretention_pa_kernel(tc, x, sin, cos, Wq_bytes, Wq_scale, Wk, out_0, out_1):

@@ -30,20 +30,20 @@ PARTS = ((0, HALF), (HALF, CHUNK))
 FLOPS = 2 * 2 * B * E * HK
 
 VECTOR = (
-    "Z Wq00.0 Wq00.1 Wq00.2 Wq01.0 Iq00 Ik00 Qq00 Iq01 Qk00 Iq02 Qq01 Ik01 xQ R0 Qq02 R1 Ik02 Qk01 Iq10 "
-    "Qk02 Iq11 Qq10 Ik10v0 Qq11 Iq12 Qk10 Ik11 Qq12 Iq20 Qk11 Ik12w Qq20 Iq21 Qk12 Iq22v0 Qq21 Ia Qq22 "
+    "Z Wq00.0 Wq00.1 Wq00.2 Wq01.0 Iq00 Ik00v0 Qq00 Iq01 Qk00 Ik01 Qq01 Iq02 Qk01 Iq10 Qq02 xQ R0 Qq10 R1 "
+    "Ik02 Iq11 Qk02 Ik10v0 Qq11 Iq12 Qk10 Ik11 Qq12 Iq20 Qk11 Ik12 Qq20 Iq21 Qk12 Iq22v0 Qq21 Ia Qq22 "
     "Ik21v0 Ib Qk20 Qk21 Qa Qb F0 F1 G0 G1"
 )
 SCALAR = (
-    "Wq00.3 Wq01.1 Wq01.2 Wq01.3 Wq02.0 Wq02.1 Wq02.2 Wq02.3 Wq10.0 Wq10.1 Wq10.2 Wq10.3 xE0 xE1 xE2 "
-    "Wq11.0 Wq11.1 Wq11.2 Wq11.3 Wq12.0 Wq12.1 Wq12.2 Wq12.3 E1q0 Ik10.1 Wq20.0 Wq20.1 Wq20.2 E1k0 E2q0 "
-    "Wq20.3 Wq21.0 Wq21.1 Wq21.2 Wq21.3 Ik12z Wq22.0 Wq22.1 Wq22.2 Wq22.3 E1q1 Iq22.1 Ik20.0 Ik20.1 E1k1 "
+    "Wq00.3 Wq01.1 Wq01.2 Wq01.3 Ik00.1 Wq02.0 Wq02.1 Wq02.2 Wq02.3 Wq10.0 Wq10.1 Wq10.2 Wq10.3 xE0 xE1 "
+    "xE2 Wq11.0 Wq11.1 Wq11.2 Wq11.3 Wq12.0 Wq12.1 Wq12.2 Wq12.3 E1q0 Ik10.1 Wq20.0 Wq20.1 Wq20.2 Wq20.3 "
+    "Wq21.0 E1k0 E2q0 Wq21.1 Wq21.2 Wq21.3 Wq22.0 Wq22.1 Wq22.2 Wq22.3 E1q1 Iq22.1 Ik20.0 Ik20.1 E1k1 "
     "Ik21.1 E1q2 C E2k0 E2q1 E2k1 E2q2a E2q2b"
 )
 TENSOR = (
     "xT B M1q0 M2q0 M1k0 M2k0 M1q1 M2q1 M1k1 M1q2 M2k1 Mpre0 Mpre1 Pa Pb M2q2a M2q2b"
 )
-LOADS = "s q00 q01 k00 q02 q10 x c k01 q11 k02 q12 k10 q20 k11 k12 q21 q22 k20 k21 k22"
+LOADS = "s q00 q01 k00 q02 k01 q10 x c q11 k02 q12 k10 q20 k11 k12 q21 q22 k20 k21 k22"
 
 
 def tile_multiscaleretention_pa_kernel(tc, x, sin, cos, Wq_bytes, Wq_scale, Wk, out_0, out_1):
@@ -317,10 +317,6 @@ def tile_multiscaleretention_pa_kernel(tc, x, sin, cos, Wq_bytes, Wq_scale, Wk, 
                 quantize(last, lo, lo + HALF)
             elif tok.startswith("I") and len(tok) == 4:
                 interleave(unit(tok[1:4]), 0, CHUNK, True)
-            elif tok.startswith("I") and tok[4] in "wz":
-                cut = 3 * CHUNK // 4
-                lo, hi = (0, cut) if tok[4] == "w" else (cut, CHUNK)
-                interleave(unit(tok[1:4]), lo, hi, tok[4] == "w")
             elif tok.startswith("I") and tok[4] == "v":
                 h = int(tok[5])
                 interleave(unit(tok[1:4]), h * CHUNK // 2, (h + 1) * CHUNK // 2, True)

from contextlib import ExitStack

import concourse.mybir as mybir
from concourse.masks import make_identity

F32 = mybir.dt.float32
BF16 = mybir.dt.bfloat16
U32 = mybir.dt.uint32
U8 = mybir.dt.uint8
FP8 = mybir.dt.float8_e4m3fn
FP8X4 = mybir.dt.float8_e4m3fn_x4
ACT = mybir.ActivationFunctionType
ALU = mybir.AluOpType

B = 128
E = 1536
HK = 1536
DK = 64
P = 128
PACK = 4
K_PASS = P * PACK
PASSES = E // K_PASS
CHUNK = 512
CHUNKS = HK // CHUNK
TILES = CHUNK // P

HALF = CHUNK // 2
PARTS = ((0, HALF), (HALF, CHUNK))

FLOPS = 2 * 2 * B * E * HK

VECTOR = (
    "Z Wq00.0 Wq00.1 Wq00.2 Wq01.0 Iq00 Ik00v0 Qq00 Iq01 Qk00 Ik01 Qq01 Iq02 Qk01 Iq10 Qq02 xQ R0 Qq10 R1 "
    "Ik02 Iq11 Qk02 Ik10v0 Qq11 Iq12 Qk10 Ik11 Qq12 Iq20 Qk11 Ik12 Qq20 Iq21 Qk12 Iq22v0 Qq21 Ia Qq22 "
    "Ik21v0 Ib Qk20 Qk21 Qa Qb F0 F1 G0 G1"
)
SCALAR = (
    "Wq00.3 Wq01.1 Wq01.2 Wq01.3 Ik00.1 Wq02.0 Wq02.1 Wq02.2 Wq02.3 Wq10.0 Wq10.1 Wq10.2 Wq10.3 xE0 xE1 "
    "xE2 Wq11.0 Wq11.1 Wq11.2 Wq11.3 Wq12.0 Wq12.1 Wq12.2 Wq12.3 E1q0 Ik10.1 Wq20.0 Wq20.1 Wq20.2 Wq20.3 "
    "Wq21.0 E1k0 E2q0 Wq21.1 Wq21.2 Wq21.3 Wq22.0 Wq22.1 Wq22.2 Wq22.3 E1q1 Iq22.1 Ik20.0 Ik20.1 E1k1 "
    "Ik21.1 E1q2 C E2k0 E2q1 E2k1 E2q2a E2q2b"
)
TENSOR = (
    "xT B M1q0 M2q0 M1k0 M2k0 M1q1 M2q1 M1k1 M1q2 M2k1 Mpre0 Mpre1 Pa Pb M2q2a M2q2b"
)
LOADS = "s q00 q01 k00 q02 k01 q10 x c q11 k02 q12 k10 q20 k11 k12 q21 q22 k20 k21 k22"


def tile_multiscaleretention_pa_kernel(tc, x, sin, cos, Wq_bytes, Wq_scale, Wk, out_0, out_1):
    nc = tc.nc
    x2d = x.rearrange("b t e -> b (t e)")
    outs = {
        "q": out_0.rearrange("b h t d -> b (h t d)"),
        "k": out_1.rearrange("b h t d -> b (h t d)"),
    }
    wk_view = Wk.rearrange("(g p t) n -> g p t n", p=P, t=PACK)
    wq_view = Wq_bytes.rearrange("(g p t) n -> g p t n", p=P, t=PACK)

    chunks = [(m, c) for c in range(CHUNKS) for m in ("q", "k")]

    with ExitStack() as ctx:
        keep = ctx.enter_context(tc.tile_pool(name="keep", bufs=1))
        wide_pool = ctx.enter_context(tc.tile_pool(name="wide", bufs=9))
        grp_pool = ctx.enter_context(tc.tile_pool(name="grp", bufs=10))
        qt_pool = ctx.enter_context(tc.tile_pool(name="qt", bufs=3))
        res_pool = ctx.enter_context(tc.tile_pool(name="res", bufs=9))
        pst = ctx.enter_context(tc.psum_pool(name="pst", bufs=3))
        ps1 = ctx.enter_context(tc.psum_pool(name="ps1", bufs=2))
        ps2 = ctx.enter_context(tc.psum_pool(name="ps2", bufs=3))

        raw = {}

        def load(u):
            m, c, g = u
            cols = slice(c * CHUNK, (c + 1) * CHUNK)
            if m == "k":
                t = keep.tile([P, PACK, CHUNK], BF16, name="kraw%d%d" % (c, g))
                nc.sync.dma_start(out=t[:], in_=wk_view[g][:, :, cols])
            else:
                t = keep.tile([P, PACK, CHUNK], U8, name="qbytes%d%d" % (c, g))
                nc.sync.dma_start(out=t[:], in_=wq_view[g][:, :, cols])
            raw[u] = t

        scl = keep.tile([P, PASSES, PACK], F32, name="scl")
        x_sb = keep.tile([P, E], BF16, name="x_sb")
        cs_row = keep.tile([P, 2 * DK], BF16, name="cs_row")
        ones = keep.tile([P, P], BF16, name="ones")
        nc.vector.memset(cs_row[:], 0.0)
        nc.vector.memset(ones[:], 1.0)

        small = nc.sync
        for s in LOADS.split():
            if s == "s":
                nc.sync.dma_start(out=scl[:], in_=Wq_scale.rearrange("(g p t) o -> p g (t o)", p=P, t=PACK))
            elif s == "x":
                nc.sync.dma_start(out=x_sb[:], in_=x2d)
            elif s == "c":
                small.dma_start(out=cs_row[0:1, 0:DK], in_=cos)
                small.dma_start(out=cs_row[0:1, DK : 2 * DK], in_=sin)
            else:
                load((s[0], int(s[1]), int(s[2])))

        idsw = keep.tile([P, 2, P], F32, name="idsw")
        make_identity(nc, idsw[:, 0, :])
        ident = idsw[:, 0, :]
        id_pairs = idsw[:, 0, :].rearrange("p (i two) -> p i two", two=2)
        sw_pairs = idsw[:, 1, :].rearrange("p (i two) -> p i two", two=2)

        warm = keep.tile([P, 2], F32, name="warm")
        nc.vector.memset(warm[:, 0:1], 0.0)
        nc.scalar.activation(out=warm[:, 1:2], in_=warm[:, 0:1], func=ACT.Copy)

        rot = keep.tile([P, P], F32, name="rot")
        x_grp = keep.tile([P, PASSES, B * PACK], BF16, name="x_grp", align_bytes=64)
        x_codes = keep.tile([P, PASSES, B], U32, name="x_codes", align_bytes=64)
        x_scales = keep.tile([P, PASSES, B], U8, name="x_scales", align_bytes=64)

        spread = {}

        prod = keep.tile([P, 2, P], F32, name="prod")

        codes = {}
        scales = {}
        for ch in chunks:
            codes[ch] = keep.tile([P, PASSES, CHUNK], U32, name="codes_%s%d" % ch, align_bytes=64)
            scales[ch] = keep.tile([P, PASSES, CHUNK], U8, name="scales_%s%d" % ch, align_bytes=64)

        wide = {}
        grp = {}
        acc = {}
        qts = {}
        turned = {}

        def unit(s):
            return (s[0], int(s[1]), int(s[2]))

        def widen(u, t, on_vector):
            if u not in wide:
                w = wide_pool.tile([P, PACK, CHUNK], BF16, name="wide")
                wide[u] = w
            g = u[2]
            if on_vector:
                nc.vector.tensor_scalar(
                    out=wide[u][:, t, :], in0=raw[u][:, t, :].bitcast(FP8), scalar1=scl[:, g, t : t + 1], scalar2=None, op0=ALU.mult
                )
            else:
                nc.scalar.activation(
                    out=wide[u][:, t, :], in_=raw[u][:, t, :].bitcast(FP8), func=ACT.Copy, scale=scl[:, g, t : t + 1]
                )

        def interleave(u, lo, hi, on_vector):
            src = raw[u] if u[0] == "k" else wide[u]
            if u not in grp:
                gt = grp_pool.tile([P, CHUNK, PACK], BF16, name="grp", align_bytes=64)
                grp[u] = gt
            dst_v = grp[u][:, lo:hi, :].rearrange("p (c i) t -> p c t i", i=8)
            src_v = src[:, :, lo:hi].rearrange("p t (c i) -> p c t i", i=8)
            if on_vector:
                nc.vector.tensor_copy(out=dst_v, in_=src_v)
            else:
                nc.scalar.copy(out=dst_v, in_=src_v)

        def quantize(u, lo, hi):
            m, c, g = u
            nc.vector.quantize_mx(
                out=codes[(m, c)][:, g, lo:hi].bitcast(FP8X4),
                scales=scales[(m, c)][:, g, lo:hi],
                in_=grp[u][:, lo:hi, :].rearrange("p n t -> p (n t)"),
            )

        def passes(ch):
            a = ps1.tile([P, CHUNK], F32, name="acc")
            acc[ch] = a
            for j in range(TILES):
                cols = slice(j * P, (j + 1) * P)
                for g in range(PASSES):
                    nc.tensor.matmul_mx(
                        out=a[:, cols],
                        lhsT=codes[ch][:, g, cols].bitcast(FP8X4),
                        lhsT_scale=scales[ch][:, g, cols],
                        rhs=x_codes[:, g, :].bitcast(FP8X4),
                        rhs_scale=x_scales[:, g, :],
                        start=(g == 0),
                        stop=(g == PASSES - 1),
                    )

        def last_passes(part, g):
            lo, hi = PARTS[part]
            if part not in acc:
                acc_t = pst.tile([P, hi - lo], F32, name="acc_t", tag="bank")
                acc[part] = acc_t
            nc.tensor.matmul_mx(
                out=acc[part][:],
                lhsT=x_codes[:, g, :].bitcast(FP8X4),
                lhsT_scale=x_scales[:, g, :],
                rhs=codes[last_ch][:, g, lo:hi].bitcast(FP8X4),
                rhs_scale=scales[last_ch][:, g, lo:hi],
                start=(g == 0),
                stop=(g == PASSES - 1),
            )

        def copy_out(ch):
            qt = qt_pool.tile([P, CHUNK], F32, name="qt")
            nc.scalar.copy(out=qt[:], in_=acc[ch][:])
            qts[ch] = qt

        def rotate(ch, tiles):
            tu = ps2.tile([P, CHUNK], F32, name="turned")
            turned[(ch, tiles[0] * P)] = tu
            for j in tiles:
                cols = slice(j * P, (j + 1) * P)
                nc.tensor.matmul(out=tu[:, cols], lhsT=qts[ch][:, cols], rhs=rot[:], start=True, stop=True)

        def store(ch, lo, hi):
            m, c = ch
            res = res_pool.tile([P, CHUNK], F32, name="res")
            nc.scalar.copy(out=res[:, lo:hi], in_=turned[(ch, lo)][:, lo:hi])
            nc.sync.dma_start(out=outs[m][:, c * CHUNK + lo : c * CHUNK + hi], in_=res[:, lo:hi])

        cs = keep.tile([P, 2, DK], F32, name="cs")

        def build_cs():
            nc.scalar.copy(out=cs[:].rearrange("p s d -> p (s d)"), in_=spread["cs"][:])
            nc.scalar.activation(out=cs[:, 1, 0:DK:2], in_=spread["cs"][:, DK : 2 * DK : 2], func=ACT.Copy, scale=-1.0)

        def products(part):
            width = acc[part].shape[1]
            heads = width // DK
            straight = keep.tile([P, width], F32, name="straight%d" % part)
            crossed = keep.tile([P, width], F32, name="crossed%d" % part)
            nc.vector.tensor_tensor(
                out=straight[:].rearrange("p (h d) -> p h d", h=heads),
                in0=acc[part][:].rearrange("p (h d) -> p h d", h=heads),
                in1=cs[:, 0, :].unsqueeze(1).to_broadcast([P, heads, DK]),
                op=ALU.mult,
            )
            nc.vector.tensor_tensor(
                out=crossed[:].rearrange("p (h i two) -> p h i two", h=heads, two=2),
                in0=acc[part][:].rearrange("p (h i two) -> p h i two", h=heads, two=2)[:, :, :, ::-1],
                in1=cs[:, 1, :].rearrange("p (i two) -> p i two", two=2).unsqueeze(1).to_broadcast([P, heads, DK // 2, 2]),
                op=ALU.mult,
            )
            terms[part] = (straight, crossed)

        def finish(part):
            m, c = last_ch
            lo, hi = PARTS[part]
            res = res_pool.tile([P, CHUNK], F32, name="res")
            nc.vector.tensor_tensor(out=res[:, lo:hi], in0=terms[part][0][:], in1=terms[part][1][:], op=ALU.add)
            nc.sync.dma_start(out=outs[m][:, c * CHUNK + lo : c * CHUNK + hi], in_=res[:, lo:hi])

        terms = {}
        last = ("k", CHUNKS - 1, PASSES - 1)
        last_ch = (last[0], last[1])
        xts = {}
        words = x_sb[:].bitcast(F32)

        def run(tok):
            if tok == "xT":
                for g in range(PASSES):
                    xt = pst.tile([P, 2, B], F32, name="xt", tag="bank")
                    xts[g] = xt
                    for u in range(2):
                        nc.tensor.transpose(xt[:, u, :], words[:, 256 * g + u : 256 * (g + 1) : 2], ident)
            elif tok.startswith("xE"):
                g = int(tok[2])
                nc.scalar.copy(
                    out=x_grp[:, g, :].bitcast(F32).rearrange("p (b u) -> p b u", u=2),
                    in_=xts[g][:].rearrange("p u b -> p b u"),
                )
            elif tok == "xQ":
                for g in range(PASSES):
                    nc.vector.quantize_mx(out=x_codes[:, g, :].bitcast(FP8X4), scales=x_scales[:, g, :], in_=x_grp[:, g, :])
            elif tok == "B":
                cs_all = pst.tile([P, 2 * DK], F32, name="cs_all", tag="bank")
                nc.tensor.matmul(out=cs_all[:], lhsT=ones[:], rhs=cs_row[:], start=True, stop=True)
                spread["cs"] = cs_all
            elif tok == "Z":
                nc.vector.tensor_scalar(out=sw_pairs[:, :, 0], in0=id_pairs[:, :, 1], scalar1=-1.0, scalar2=None, op0=ALU.mult)
                nc.vector.tensor_copy(out=sw_pairs[:, :, 1], in_=id_pairs[:, :, 0])
            elif tok == "R0":
                nc.vector.tensor_tensor(
                    out=prod[:].rearrange("p s (h d) -> p s h d", h=2),
                    in0=idsw[:].rearrange("p s (h d) -> p s h d", h=2),
                    in1=spread["cs"][:].rearrange("p (s d) -> p s d", s=2).unsqueeze(2).to_broadcast([P, 2, 2, DK]),
                    op=ALU.mult,
                )
            elif tok == "R1":
                nc.vector.tensor_tensor(out=rot[:], in0=prod[:, 0, :], in1=prod[:, 1, :], op=ALU.add)
            elif tok == "C":
                build_cs()
            elif tok.startswith("F"):
                products(int(tok[1]))
            elif tok.startswith("G"):
                finish(int(tok[1]))
            elif tok.startswith("Mpre"):
                for part in range(len(PARTS)):
                    last_passes(part, int(tok[4]))
            elif tok in ("Pa", "Pb"):
                last_passes("ab".index(tok[1]), PASSES - 1)
            elif tok.startswith("M1"):
                passes((tok[2], int(tok[3])))
            elif tok.startswith("E1"):
                copy_out((tok[2], int(tok[3])))
            elif tok.startswith("M2"):
                rotate((tok[2], int(tok[3])), {"": (0, 1, 2, 3), "a": (0, 1), "b": (2, 3)}[tok[4:]])
            elif tok.startswith("E2"):
                lo, hi = {"": (0, CHUNK), "a": (0, HALF), "b": (HALF, CHUNK)}[tok[4:]]
                store((tok[2], int(tok[3])), lo, hi)
            elif tok.startswith("W"):
                widen(unit(tok[1:4]), int(tok[5]), tok in VECTOR.split())
            elif tok in ("Ia", "Ib"):
                lo = HALF * (tok == "Ib")
                interleave(last, lo, lo + HALF, True)
            elif tok in ("Qa", "Qb"):
                lo = HALF * (tok == "Qb")
                quantize(last, lo, lo + HALF)
            elif tok.startswith("I") and len(tok) == 4:
                interleave(unit(tok[1:4]), 0, CHUNK, True)
            elif tok.startswith("I") and tok[4] == "v":
                h = int(tok[5])
                interleave(unit(tok[1:4]), h * CHUNK // 2, (h + 1) * CHUNK // 2, True)
            elif tok.startswith("I"):
                h = int(tok[5])
                interleave(unit(tok[1:4]), h * CHUNK // 2, (h + 1) * CHUNK // 2, False)
            elif tok.startswith("Q"):
                quantize(unit(tok[1:4]), 0, CHUNK)
            else:
                raise ValueError(tok)

        queues = [VECTOR.split(), SCALAR.split(), TENSOR.split()]
        names = [q for queue in queues for q in queue]
        written = set()

        turns = [n[2:] for n in TENSOR.split() if n.startswith("M2")]

        def needs(tok):
            u = tok[1:4]
            if tok.startswith("xE"):
                return ["xT"]
            if tok == "xQ":
                return ["xE%d" % g for g in range(PASSES)]
            if tok == "R0":
                return ["B", "Z"]
            if tok == "R1":
                return ["R0"]
            if tok == "C":
                return ["B"]
            if tok.startswith("Iq"):
                return [n for n in names if n.startswith("W" + u)]
            if tok.startswith("Qq") or tok.startswith("Qk"):
                return [n for n in names if n.startswith("I" + u)]
            if tok.startswith("Q"):
                return ["I" + tok[1]]
            if tok.startswith("Mpre"):
                return ["xQ", "Q%s%d%s" % (last_ch[0], last_ch[1], tok[4])]
            if tok.startswith("P"):
                return ["Mpre1", "Q" + tok[1]]
            if tok.startswith("M1"):
                older = chunks.index((tok[2], int(tok[3]))) - 2
                return ["xQ"] + ["Q%s%d" % (tok[2:4], g) for g in range(PASSES)] + (["E1%s%d" % chunks[older]] if older >= 0 else [])
            if tok.startswith("M2"):
                older = turns.index(tok[2:]) - 3
                return ["E1" + tok[2:4], "R1"] + (["E2" + turns[older]] if older >= 0 else [])
            if tok == "B":
                return ["xE0"]
            if tok.startswith("E"):
                return ["M" + tok[1:]]
            if tok.startswith("F"):
                return ["C", "P" + "ab"[int(tok[1])]]
            if tok.startswith("G"):
                return ["F" + tok[1]]
            return []

        with tc.manual_schedule():
            at = [0, 0, 0]
            while len(written) < len(names):
                before = len(written)
                for e, queue in enumerate(queues):
                    if at[e] < len(queue) and all(n in written for n in needs(queue[at[e]])):
                        run(queue[at[e]])
                        written.add(queue[at[e]])
                        at[e] = at[e] + 1
                assert len(written) > before
